import numpy as np
import ml_dtypes


def mxq(x, axis, fmt="e4m3"):
    dtype, down = {"e4m3": (ml_dtypes.float8_e4m3fn, 7), "e5m2": (ml_dtypes.float8_e5m2, 14)}[fmt]
    v = np.moveaxis(np.asarray(x, np.float32).astype(ml_dtypes.bfloat16).astype(np.float64), axis, -1)
    blocks = v.reshape(v.shape[:-1] + (-1, 32))
    amax = np.abs(blocks).max(-1, keepdims=True)
    byte = np.maximum(np.where(amax > 0, np.frexp(amax)[1] - 1 + 127, 0) - down, 1)
    scale = np.exp2(byte - 127.0)
    codes = (blocks / scale).astype(np.float32).astype(dtype).astype(np.float64)
    return np.moveaxis((codes * scale).reshape(v.shape), -1, axis)


WIDE = False


def mx_kscale(k):
    if not WIDE:
        return np.ones(k)
    levels = np.array([18, -18])
    if k % 512:
        return np.exp2(np.random.permutation(np.resize(levels, k // 32))).repeat(32)
    a = np.empty((k // 512, 16))
    for p in range(k // 512):
        a[p, :8] = np.random.permutation(np.resize(levels, 8))
        for g in range(8):
            far = levels[np.abs(levels - a[p, g]) >= 10]
            a[p, g + 8] = far[np.random.randint(len(far))]
    return np.exp2(a.ravel()).repeat(32)


BF16 = ml_dtypes.bfloat16


def bf(x):
    return np.asarray(x, np.float32).astype(BF16)


def f64(x):
    return np.asarray(x).astype(np.float64)


B, S, H, F = 128, 8, 512, 512


def preactivations(h, ew1, eb1):
    left, right = h[:, :-1, :], h[:, 1:, :]
    z_lr = np.concatenate([left, right], axis=-1) @ ew1 + eb1
    z_rl = np.concatenate([right, left], axis=-1) @ ew1 + eb1
    return z_lr, z_rl


def setup_inputs():
    s = np.repeat(mx_kscale(B * S)[::S], S).reshape(B, S, 1)
    u = mx_kscale(H)
    v = mx_kscale(F)
    h0 = bf(np.random.standard_normal((B, S, H)))
    ew1_0 = bf(np.random.standard_normal((2 * H, F)) / np.sqrt(2 * H))
    eb1 = bf(np.random.standard_normal(F) * 0.3)
    ew2_0 = bf(np.random.standard_normal((F, H)) / np.sqrt(F))
    eb2 = bf(np.random.standard_normal(H) * 0.3)
    g = bf(np.random.standard_normal((B, S, H)) * np.exp2(np.random.randint(-6, 1, (B, S, 1))) / s * u)
    z_lr, z_rl = preactivations(f64(h0), f64(ew1_0), f64(eb1))
    return {"h": bf(f64(h0) * s), "ew1": bf(f64(ew1_0) / v), "eb1": eb1,
            "ew2": bf(f64(ew2_0) * v[:, None] / u), "eb2": eb2,
            "z_lr": np.asarray(z_lr, np.float32), "z_rl": np.asarray(z_rl, np.float32), "grad_out": g}


def reference(h, ew1, eb1, ew2, eb2, z_lr, z_rl, grad_out):
    T = B * S
    g = f64(grad_out).reshape(T, H)
    d = (mxq(g, 1, "e5m2") @ mxq(f64(ew2), 1, "e4m3").T).reshape(B, S, F)
    dz_lr = np.where(f64(z_lr) > 0.0, d[:, 1:, :], 0.0)
    dz_rl = np.where(f64(z_rl) > 0.0, d[:, :-1, :], 0.0)
    zrow = np.zeros((B, 1, F))
    a = np.concatenate([dz_lr, zrow], axis=1) + np.concatenate([zrow, dz_rl], axis=1)
    c = np.concatenate([zrow, dz_lr], axis=1) + np.concatenate([dz_rl, zrow], axis=1)
    dz1 = np.concatenate([a, c], axis=2).reshape(T, 2 * F)
    w = np.concatenate([f64(ew1)[:H], f64(ew1)[H:]], axis=1)
    dx = mxq(dz1, 1, "e5m2") @ mxq(w, 1, "e4m3").T
    dw = mxq(f64(h).reshape(T, H), 0, "e4m3").T @ mxq(dz1, 0, "e5m2")
    dew1 = np.concatenate([dw[:, :F], dw[:, F:]], axis=0)
    return dx.reshape(B, S, H), dew1

@@ -1,0 +1,384 @@
+from contextlib import ExitStack
+
+import concourse.mybir as mybir
+from concourse.masks import make_identity
+
+F32 = mybir.dt.float32
+BF16 = mybir.dt.bfloat16
+U32 = mybir.dt.uint32
+U8 = mybir.dt.uint8
+E4M3 = mybir.dt.float8_e4m3fn_x4
+E5M2 = mybir.dt.float8_e5m2_x4
+ALU = mybir.AluOpType
+
+P = 128
+CHAINS, NODES, H, F = 128, 8, 512, 512
+HALF = NODES // 2
+FLOPS = 2 * CHAINS * NODES * H * F * 5
+BYTES = 2 * (2 * 1024 * 512 + 1024 * 512 + 512 * 512) + 4 * 2 * 128 * 7 * 512 + 4 * 2 * 1024 * 512
+
+STORE = {0: 0, 3: 1, 1: 2, 2: 3, 4: 4}
+
+
+def tile_graphnetlayer_pa_v_kernel(tc, h, ew1, eb1, ew2, eb2, z_lr, z_rl, grad_out, out_0, out_1):
+    nc = tc.nc
+    with ExitStack() as ctx:
+        sb = ctx.enter_context(tc.tile_pool(name="sb", bufs=1))
+        ps = ctx.enter_context(tc.psum_pool(name="ps", bufs=1))
+        ctx.enter_context(tc.manual_schedule())
+
+        groups = {"d": [0, 1, 2, 3, 4], "w": [5, 6, 7], "all": [0, 1, 2, 3, 4, 5, 6, 7]}
+        turn = {"d": 0, "w": 0, "all": 0}
+
+        def bank(group):
+            i = groups[group][turn[group] % len(groups[group])]
+            turn[group] += 1
+            b = ps.tile([P, 512], F32, name="bank%d" % i)
+            return b
+
+        def copy(eng, out, in_):
+            if eng == "S":
+                nc.scalar.copy(out=out, in_=in_)
+            else:
+                nc.vector.tensor_copy(out=out, in_=in_)
+
+        def quant(codes, scales, grouped, fmt):
+            nc.vector.quantize_mx(out=codes.bitcast(fmt), scales=scales, in_=grouped)
+
+        def flat(t):
+            return t.rearrange("q n t -> q (n t)")
+
+        ew2_sb = sb.tile([P, 4, H], BF16, name="ew2_sb", align_bytes=64)
+        ew1_sb = sb.tile([P, 8, F], BF16, name="ew1_sb", align_bytes=64)
+        h_sb = sb.tile([P, 2, HALF, H], BF16, name="h_sb", align_bytes=64)
+        g_sb = [sb.tile([P, HALF, H], BF16, name="g_sb%d" % x, align_bytes=64) for x in range(2)]
+        zx = [sb.tile([P, HALF, F], F32, name="zx%d" % x, align_bytes=64) for x in range(2)]
+        zy = [sb.tile([P, HALF, F], F32, name="zy%d" % x, align_bytes=64) for x in range(2)]
+
+        g_view = grad_out.rearrange("(x c) (n t) h -> x (c n) t h", x=2, n=2)
+        h_view = h.rearrange("(x c) n h -> c x n h", x=2)
+        lr_view = z_lr.rearrange("(x c) e f -> x c e f", x=2)
+        rl_view = z_rl.rearrange("(x c) e f -> x c e f", x=2)
+        ew2_view = ew2.rearrange("(i p) h -> p i h", p=P)
+        ew1_view = ew1.rearrange("(i p) f -> p i f", p=P)
+
+        def load(out, in_):
+            nc.sync.dma_start(out=out, in_=in_)
+
+        def load_g(x):
+            load(g_sb[x][:, 0::3, :], g_view[x][:, 0::3, :])
+            load(g_sb[x][:, 1:3, :], g_view[x][:, 1:3, :])
+
+        def load_z(x, j):
+            load(zy[x][1::2, j, :], lr_view[x][:, 6 - j, :])
+            if j % 2 == 0:
+                load(zy[x][0::2, j : j + 2, :], rl_view[x][:, j : j + 2, :])
+            load(zx[x][1::2, j, :], rl_view[x][:, 6 - j, :])
+            if j % 2 == 0:
+                load(zx[x][0::2, j : j + 2, :], lr_view[x][:, j : j + 2, :])
+
+        def load_h(x):
+            load(h_sb[0::2, x], h_view[:, x, 0:4, :])
+            for j in range(4):
+                load(h_sb[1::2, x, j, :], h_view[:, x, 7 - j, :])
+
+        load(ew2_sb[:, 0:2, :], ew2_view[:, 0:2, :])
+        load(ew2_sb[:, 2:4, :], ew2_view[:, 2:4, :])
+        load_g(0)
+        load_z(0, 0)
+        load_z(0, 1)
+        load_h(0)
+        load_z(0, 2)
+        load_z(0, 3)
+        load_h(1)
+        load(ew1_sb[:, 0:4, :], ew1_view[:, 0:4, :])
+        load(ew1_sb[:, 4:8, :], ew1_view[:, 4:8, :])
+        load_g(1)
+        load_z(1, 0)
+        load_z(1, 1)
+        load_z(1, 2)
+        load_z(1, 3)
+
+        ident = sb.tile([P, P], F32, name="ident", align_bytes=64)
+        perm = sb.tile([P, P], F32, name="perm", align_bytes=64)
+        make_identity(nc, ident[:])
+        nc.vector.tensor_copy(out=perm[:].rearrange("p (n c) -> p n c", n=2), in_=ident[:].rearrange("p (c n) -> p n c", n=2))
+
+        e_grp = sb.tile([P, 512, 4], BF16, name="e_grp", align_bytes=64)
+        e_cod = sb.tile([P, 512], U32, name="e_cod", align_bytes=64)
+        e_scl = sb.tile([P, 512], U8, name="e_scl", align_bytes=64)
+        w_grp = [sb.tile([P, 512, 4], BF16, name="w_grp%d" % a, align_bytes=64) for a in range(2)]
+        w_cod = [sb.tile([P, 512], U32, name="w_cod%d" % a, align_bytes=64) for a in range(2)]
+        w_scl = [sb.tile([P, 512], U8, name="w_scl%d" % a, align_bytes=64) for a in range(2)]
+
+        def weight_bank(src, i, grp, r, eng, group):
+            b = bank(group)
+            for d in range(2):
+                words = src[:, i + d, :].bitcast(F32)
+                for u in range(2):
+                    nc.tensor.transpose(b[:, d * 256 + u * 128 : d * 256 + u * 128 + 128], words[:, u::2], ident[:])
+            dst = flat(grp[:]).bitcast(F32)[:, r * 512 : (r + 1) * 512]
+            copy(eng, dst.rearrange("q (d p u) -> q d p u", d=2, u=2), b[:].rearrange("q (d u p) -> q d p u", d=2, u=2))
+
+        g_grp = [sb.tile([P, 5 * P, 4], BF16, name="g_grp%d" % x, align_bytes=64) for x in range(2)]
+        g_cod = [sb.tile([P, 5 * P], U32, name="g_cod%d" % x, align_bytes=64) for x in range(2)]
+        g_scl = [sb.tile([P, 5 * P], U8, name="g_scl%d" % x, align_bytes=64) for x in range(2)]
+
+        def pair_transposes(src0, src1, group):
+            b = bank(group)
+            for k, s in ((0, src0), (1, src1)):
+                words = s.bitcast(F32)
+                for u in range(2):
+                    nc.tensor.transpose(b[:, u * 256 + k * 128 : u * 256 + k * 128 + 128], words[:, u::2], perm[:])
+            return b
+
+        EVEN0_ODD1 = slice(0, 4, 3)
+        EVEN1_ODD0 = slice(2, 0, -1)
+        ODD0_EVEN1 = slice(1, 3)
+
+        def diag_copy(eng, b, sel, dst_cols):
+            src_v = b[:].rearrange("q (u m c) -> q u m c", u=2, m=4)[:, :, sel, :].rearrange("q u n c -> q c n u")
+            dst_v = flat(dst_cols).bitcast(F32).rearrange("q (c n u) -> q c n u", n=2, u=2)
+            copy(eng, dst_v, src_v)
+
+        def tile_cols(slot):
+            s = STORE[slot]
+            return slice(s * P, (s + 1) * P)
+
+        def g_bank(x, k, group):
+            return pair_transposes(g_sb[x][:, k, :], g_sb[x][:, 3 - k, :], group)
+
+        def g_copies(x, k, b, engs):
+            diag_copy(engs[0], b, EVEN0_ODD1, g_grp[x][:, tile_cols(k), :])
+            diag_copy(engs[1], b, EVEN1_ODD0, g_grp[x][:, tile_cols(3 - k), :])
+            if k == 0:
+                diag_copy(engs[2], b, ODD0_EVEN1, g_grp[x][:, tile_cols(4), :])
+
+        def g_quant(x, lo, hi):
+            c = slice(lo * P, hi * P)
+            quant(g_cod[x][:, c], g_scl[x][:, c], flat(g_grp[x][:, c, :]), E5M2)
+
+        def d_bank(x, slot):
+            b = bank("d")
+            c = tile_cols(slot)
+            nc.tensor.matmul_mx(out=b[:], lhsT=g_cod[x][:, c].bitcast(E5M2), lhsT_scale=g_scl[x][:, c],
+                                rhs=e_cod[:].bitcast(E4M3), rhs_scale=e_scl[:], start=True, stop=True)
+            return b
+
+        xs = [sb.tile([P, HALF, F], F32, name="xs%d" % x, align_bytes=64) for x in range(2)]
+        ys = [sb.tile([P, HALF, F], F32, name="ys%d" % x, align_bytes=64) for x in range(2)]
+        ac = [sb.tile([P, 2, HALF, F], BF16, name="ac%d" % x, align_bytes=64) for x in range(2)]
+
+        def mask_y(x, j, d, f):
+            nc.vector.scalar_tensor_tensor(out=ys[x][:, j, f], in0=zy[x][:, j, f], scalar=0.0, in1=d[j][:, f], op0=ALU.is_gt, op1=ALU.mult)
+
+        def mask_x(x, j, d, f):
+            nc.vector.scalar_tensor_tensor(out=xs[x][:, j, f], in0=zx[x][:, j, f], scalar=0.0, in1=d[j + 1][:, f], op0=ALU.is_gt, op1=ALU.mult)
+
+        def sums(x, lo, hi, f):
+            nc.vector.tensor_tensor(out=ac[x][:, 1, lo:hi, f], in0=xs[x][:, lo - 1 : hi - 1, f], in1=ys[x][:, lo:hi, f], op=ALU.add)
+            nc.vector.tensor_tensor(out=ac[x][:, 0, lo:hi, f], in0=xs[x][:, lo:hi, f], in1=ys[x][:, lo - 1 : hi - 1, f], op=ALU.add)
+
+        def ends(x, f):
+            nc.scalar.copy(out=ac[x][:, 1, 0, f], in_=ys[x][:, 0, f])
+            nc.scalar.copy(out=ac[x][:, 0, 0, f], in_=xs[x][:, 0, f])
+
+        ALL = slice(0, F)
+        LO = slice(0, F // 2)
+        HI = slice(F // 2, F)
+        FH = (LO, HI)
+
+        t_cod = [[sb.tile([P, 512], U32, name="t_cod%d%d" % (x, a), align_bytes=64) for a in range(2)] for x in range(2)]
+        t_scl = [[sb.tile([P, 512], U8, name="t_scl%d%d" % (x, a), align_bytes=64) for a in range(2)] for x in range(2)]
+        f_cod = [[sb.tile([P, 512], U32, name="f_cod%d%d" % (x, a), align_bytes=64) for a in range(2)] for x in range(2)]
+        f_scl = [[sb.tile([P, 512], U8, name="f_scl%d%d" % (x, a), align_bytes=64) for a in range(2)] for x in range(2)]
+
+        def token_tile():
+            t_grp = sb.tile([P, 2, F // 2, 4], BF16, name="t_grp", tag="t_grp", bufs=3, align_bytes=64)
+            return t_grp
+
+        def token_group(t_grp, x, fh, a, eng):
+            copy(eng, t_grp[:, a].rearrange("p (c i) j -> p c j i", i=4), ac[x][:, a, :, FH[fh]].rearrange("p j (c i) -> p c j i", i=4))
+
+        def token_quant(x, fh, t_grp):
+            quant(t_cod[x][fh][:], t_scl[x][fh][:], t_grp[:].rearrange("p a f j -> p (a f j)"), E5M2)
+
+        def feat_tile(x, a):
+            f_grp = sb.tile([P, 512, 4], BF16, name="f_grp", tag="f_grp", bufs=2, align_bytes=64)
+            return f_grp
+
+        def feat_bank(x, a, k, group):
+            return pair_transposes(ac[x][:, a, k, :], ac[x][:, a, 3 - k, :], group)
+
+        def feat_copies(f_grp, k, b, engs):
+            diag_copy(engs[0], b, EVEN0_ODD1, f_grp[:, tile_cols(k), :])
+            diag_copy(engs[1], b, EVEN1_ODD0, f_grp[:, tile_cols(3 - k), :])
+
+        def feat_quant(x, a, f_grp, lo=0, hi=4):
+            c = slice(lo * P, hi * P)
+            quant(f_cod[x][a][:, c], f_scl[x][a][:, c], flat(f_grp[:, c, :]), E5M2)
+
+        h_grp = [sb.tile([P, 512, 4], BF16, name="h_grp%d" % x, align_bytes=64) for x in range(2)]
+        h_cod = [sb.tile([P, 512], U32, name="h_cod%d" % x, align_bytes=64) for x in range(2)]
+        h_scl = [sb.tile([P, 512], U8, name="h_scl%d" % x, align_bytes=64) for x in range(2)]
+
+        def h_group(x, eng):
+            copy(eng, h_grp[x][:].rearrange("p (c i) j -> p c j i", i=4), h_sb[:, x, :, :].rearrange("p j (c i) -> p c j i", i=4))
+
+        def h_quant(x):
+            quant(h_cod[x][:], h_scl[x][:], flat(h_grp[x][:]), E4M3)
+
+        out0_view = out_0.rearrange("(x c) (n m) h -> x (c n) m h", x=2, n=2)
+        out1_view = out_1.rearrange("(a m p) f -> p m a f", a=2, p=P)
+        o0 = [sb.tile([P, 4, H], F32, name="o0_%d" % x, align_bytes=64) for x in range(2)]
+
+        def out0_mx(b, x, m, a):
+            c = tile_cols(m)
+            nc.tensor.matmul_mx(out=b[:], lhsT=f_cod[x][a][:, c].bitcast(E5M2), lhsT_scale=f_scl[x][a][:, c],
+                                rhs=w_cod[a][:].bitcast(E4M3), rhs_scale=w_scl[a][:], start=(a == 0), stop=(a == 1))
+
+        def out0_end(b, x, m, eng):
+            copy(eng, o0[x][:, m, :], b[:])
+            nc.sync.dma_start(out=out0_view[x][:, m, :], in_=o0[x][:, m, :])
+
+        def out1_mx(b, fh, m, x):
+            c = slice(m * P, (m + 1) * P)
+            nc.tensor.matmul_mx(out=b[:], lhsT=h_cod[x][:, c].bitcast(E4M3), lhsT_scale=h_scl[x][:, c],
+                                rhs=t_cod[x][fh][:].bitcast(E5M2), rhs_scale=t_scl[x][fh][:], start=(x == 0), stop=(x == 1))
+
+        def out1_end(b, fh, m, eng):
+            o = sb.tile([P, 2, F // 2], F32, name="o1", tag="o1", bufs=4, align_bytes=64)
+            copy(eng, o[:].rearrange("p a f -> p (a f)"), b[:])
+            nc.sync.dma_start(out=out1_view[:, m, :, FH[fh]], in_=o[:])
+
+        weight_bank(ew2_sb, 0, e_grp, 0, "S", "all")
+        weight_bank(ew2_sb, 2, e_grp, 1, "V", "all")
+        b0 = g_bank(0, 0, "all")
+        b1 = g_bank(0, 1, "all")
+        g_copies(0, 0, b0, "VSS")
+        g_copies(0, 1, b1, "SS")
+        quant(e_cod[:], e_scl[:], flat(e_grp[:]), E4M3)
+        g_quant(0, 0, 2)
+        d = [d_bank(0, 0)]
+        g_quant(0, 2, 4)
+        d.append(d_bank(0, 1))
+        g_quant(0, 4, 5)
+        mask_y(0, 0, d, ALL)
+        d.append(d_bank(0, 2))
+        d.append(d_bank(0, 3))
+        d.append(d_bank(0, 4))
+        mask_x(0, 0, d, ALL)
+        ends(0, ALL)
+        mask_y(0, 1, d, ALL)
+        mask_x(0, 1, d, ALL)
+        sums(0, 1, 2, ALL)
+        h_group(0, "S")
+        mask_y(0, 2, d, ALL)
+        mask_x(0, 2, d, ALL)
+        sums(0, 2, 3, ALL)
+        f0 = [feat_tile(0, 0), feat_tile(0, 1)]
+        h_group(1, "S")
+        for a in range(2):
+            b = feat_bank(0, a, 1, "d")
+            feat_copies(f0[a], 1, b, "SS")
+        mask_y(0, 3, d, ALL)
+        mask_x(0, 3, d, ALL)
+        sums(0, 3, 4, ALL)
+        for a in range(2):
+            b = feat_bank(0, a, 0, "d")
+            feat_copies(f0[a], 0, b, "SS")
+        t0 = token_tile()
+        t1 = token_tile()
+        token_group(t0, 0, 0, 1, "V")
+        token_group(t0, 0, 0, 0, "V")
+        b0 = g_bank(1, 0, "d")
+        b1 = g_bank(1, 1, "d")
+        g_copies(1, 0, b0, "SSS")
+        g_copies(1, 1, b1, "SS")
+        weight_bank(ew1_sb, 0, w_grp[0], 0, "S", "w")
+        weight_bank(ew1_sb, 2, w_grp[0], 1, "S", "w")
+        weight_bank(ew1_sb, 4, w_grp[1], 0, "S", "w")
+        feat_quant(0, 0, f0[0])
+        feat_quant(0, 1, f0[1])
+        token_quant(0, 0, t0)
+        g_quant(1, 0, 2)
+        g_quant(1, 2, 4)
+        g_quant(1, 4, 5)
+        d = [d_bank(1, s) for s in range(5)]
+        weight_bank(ew1_sb, 6, w_grp[1], 1, "S", "w")
+        mask_y(1, 0, d, LO)
+        mask_x(1, 0, d, LO)
+        ends(1, LO)
+        token_group(t1, 0, 1, 0, "S")
+        token_group(t1, 0, 1, 1, "S")
+        mask_y(1, 1, d, LO)
+        mask_x(1, 1, d, LO)
+        quant(w_cod[0][:], w_scl[0][:], flat(w_grp[0][:]), E4M3)
+        mask_y(1, 2, d, LO)
+        mask_x(1, 2, d, LO)
+        quant(w_cod[1][:], w_scl[1][:], flat(w_grp[1][:]), E4M3)
+        for m in range(4):
+            b = bank("w")
+            out0_mx(b, 0, m, 0)
+            out0_mx(b, 0, m, 1)
+            out0_end(b, 0, m, "S")
+        mask_y(1, 3, d, LO)
+        mask_x(1, 3, d, LO)
+        h_quant(0)
+        sums(1, 1, 4, LO)
+        h_quant(1)
+        t0 = token_tile()
+        token_group(t0, 1, 0, 1, "S")
+        token_group(t0, 1, 0, 0, "V")
+        mask_y(1, 0, d, HI)
+        mask_x(1, 0, d, HI)
+        ends(1, HI)
+        mask_y(1, 1, d, HI)
+        mask_x(1, 1, d, HI)
+        token_quant(1, 0, t0)
+        for m in range(4):
+            b = bank("w")
+            out1_mx(b, 0, m, 0)
+            out1_mx(b, 0, m, 1)
+            out1_end(b, 0, m, "S")
+        mask_y(1, 2, d, HI)
+        mask_x(1, 2, d, HI)
+        sums(1, 1, 3, HI)
+        f1 = [feat_tile(1, 0), feat_tile(1, 1)]
+        for a in range(2):
+            b = feat_bank(1, a, 1, "w")
+            feat_copies(f1[a], 1, b, "SS")
+        mask_y(1, 3, d, HI)
+        mask_x(1, 3, d, HI)
+        token_quant(0, 1, t1)
+        sums(1, 3, 4, HI)
+        t1 = token_tile()
+        token_group(t1, 1, 1, 1, "V")
+        feat_quant(1, 0, f1[0], 2, 4)
+        feat_quant(1, 1, f1[1], 2, 4)
+        token_group(t1, 1, 1, 0, "V")
+        for a in range(2):
+            b = feat_bank(1, a, 0, "w")
+            feat_copies(f1[a], 0, b, "SS")
+        bf = [None] * 4
+        for m in (1, 2):
+            bf[m] = bank("all")
+            out0_mx(bf[m], 1, m, 0)
+            out0_mx(bf[m], 1, m, 1)
+            out0_end(bf[m], 1, m, "S")
+        bt = [bank("all") for m in range(4)]
+        for m in range(4):
+            out1_mx(bt[m], 1, m, 0)
+        token_quant(1, 1, t1)
+        for m in range(4):
+            out1_mx(bt[m], 1, m, 1)
+        feat_quant(1, 0, f1[0], 0, 2)
+        feat_quant(1, 1, f1[1], 0, 2)
+        for m in (0, 3):
+            bf[m] = bank("all")
+            out0_mx(bf[m], 1, m, 0)
+            out0_mx(bf[m], 1, m, 1)
+        for m in range(4):
+            out1_end(bt[m], 1, m, "SV"[m % 2])
+        out0_end(bf[0], 1, 0, "S")
+        out0_end(bf[3], 1, 3, "V")

@@ -27,12 +27,7 @@ def tile_graphnetlayer_pa_v_kernel(tc, h, ew1, eb1, ew2, eb2, z_lr, z_rl, grad_o
         ps = ctx.enter_context(tc.psum_pool(name="ps", bufs=1))
         ctx.enter_context(tc.manual_schedule())
 
-        groups = {"d": [0, 1, 2, 3, 4], "w": [5, 6, 7], "all": [0, 1, 2, 3, 4, 5, 6, 7]}
-        turn = {"d": 0, "w": 0, "all": 0}
-
-        def bank(group):
-            i = groups[group][turn[group] % len(groups[group])]
-            turn[group] += 1
+        def bank(i):
             b = ps.tile([P, 512], F32, name="bank%d" % i)
             return b
 
@@ -44,6 +39,16 @@ def tile_graphnetlayer_pa_v_kernel(tc, h, ew1, eb1, ew2, eb2, z_lr, z_rl, grad_o
 
         def quant(codes, scales, grouped, fmt):
             nc.vector.quantize_mx(out=codes.bitcast(fmt), scales=scales, in_=grouped)
+
+        zz = sb.tile([P, 512], BF16, name="zz", align_bytes=64)
+        nc.vector.memset(zz[:], 0.0)
+
+        def warm(b, plain, mx):
+            for i in range(plain):
+                nc.tensor.matmul(out=b[:], lhsT=zz[:, 0:P], rhs=zz[:], start=True, stop=True)
+            for i in range(mx):
+                nc.tensor.matmul_mx(out=b[:], lhsT=g_cod[0][:, 0:P].bitcast(E5M2), lhsT_scale=g_scl[0][:, 0:P],
+                                    rhs=e_cod[:].bitcast(E4M3), rhs_scale=e_scl[:], start=True, stop=True)
 
         def flat(t):
             return t.rearrange("q n t -> q (n t)")
@@ -87,13 +92,13 @@ def tile_graphnetlayer_pa_v_kernel(tc, h, ew1, eb1, ew2, eb2, z_lr, z_rl, grad_o
         load_g(0)
         load_z(0, 0)
         load_z(0, 1)
-        load_h(0)
+        load_g(1)
         load_z(0, 2)
+        load_h(0)
         load_z(0, 3)
-        load_h(1)
         load(ew1_sb[:, 0:4, :], ew1_view[:, 0:4, :])
         load(ew1_sb[:, 4:8, :], ew1_view[:, 4:8, :])
-        load_g(1)
+        load_h(1)
         load_z(1, 0)
         load_z(1, 1)
         load_z(1, 2)
@@ -111,8 +116,9 @@ def tile_graphnetlayer_pa_v_kernel(tc, h, ew1, eb1, ew2, eb2, z_lr, z_rl, grad_o
         w_cod = [sb.tile([P, 512], U32, name="w_cod%d" % a, align_bytes=64) for a in range(2)]
         w_scl = [sb.tile([P, 512], U8, name="w_scl%d" % a, align_bytes=64) for a in range(2)]
 
-        def weight_bank(src, i, grp, r, eng, group):
-            b = bank(group)
+        def weight_bank(src, i, grp, r, eng, i_bank, plain=0, mx=0):
+            b = bank(i_bank)
+            warm(b, plain, mx)
             for d in range(2):
                 words = src[:, i + d, :].bitcast(F32)
                 for u in range(2):
@@ -124,12 +130,12 @@ def tile_graphnetlayer_pa_v_kernel(tc, h, ew1, eb1, ew2, eb2, z_lr, z_rl, grad_o
         g_cod = [sb.tile([P, 5 * P], U32, name="g_cod%d" % x, align_bytes=64) for x in range(2)]
         g_scl = [sb.tile([P, 5 * P], U8, name="g_scl%d" % x, align_bytes=64) for x in range(2)]
 
-        def pair_transposes(src0, src1, group):
-            b = bank(group)
-            for k, s in ((0, src0), (1, src1)):
-                words = s.bitcast(F32)
+        def pair_transposes(words, i_bank, plain=0, mx=0):
+            b = bank(i_bank)
+            warm(b, plain, mx)
+            for k in range(2):
                 for u in range(2):
-                    nc.tensor.transpose(b[:, u * 256 + k * 128 : u * 256 + k * 128 + 128], words[:, u::2], perm[:])
+                    nc.tensor.transpose(b[:, u * 256 + k * 128 : u * 256 + k * 128 + 128], words[k][u], perm[:])
             return b
 
         EVEN0_ODD1 = slice(0, 4, 3)
@@ -145,8 +151,8 @@ def tile_graphnetlayer_pa_v_kernel(tc, h, ew1, eb1, ew2, eb2, z_lr, z_rl, grad_o
             s = STORE[slot]
             return slice(s * P, (s + 1) * P)
 
-        def g_bank(x, k, group):
-            return pair_transposes(g_sb[x][:, k, :], g_sb[x][:, 3 - k, :], group)
+        def g_bank(x, k, i_bank, plain=0, mx=0):
+            return pair_transposes([[g_sb[x][:, s, :].bitcast(F32)[:, u::2] for u in range(2)] for s in (k, 3 - k)], i_bank, plain, mx)
 
         def g_copies(x, k, b, engs):
             diag_copy(engs[0], b, EVEN0_ODD1, g_grp[x][:, tile_cols(k), :])
@@ -158,8 +164,9 @@ def tile_graphnetlayer_pa_v_kernel(tc, h, ew1, eb1, ew2, eb2, z_lr, z_rl, grad_o
             c = slice(lo * P, hi * P)
             quant(g_cod[x][:, c], g_scl[x][:, c], flat(g_grp[x][:, c, :]), E5M2)
 
-        def d_bank(x, slot):
-            b = bank("d")
+        def d_bank(x, slot, i_bank, plain=0, mx=0):
+            b = bank(i_bank)
+            warm(b, plain, mx)
             c = tile_cols(slot)
             nc.tensor.matmul_mx(out=b[:], lhsT=g_cod[x][:, c].bitcast(E5M2), lhsT_scale=g_scl[x][:, c],
                                 rhs=e_cod[:].bitcast(E4M3), rhs_scale=e_scl[:], start=True, stop=True)
@@ -167,7 +174,7 @@ def tile_graphnetlayer_pa_v_kernel(tc, h, ew1, eb1, ew2, eb2, z_lr, z_rl, grad_o
 
         xs = [sb.tile([P, HALF, F], F32, name="xs%d" % x, align_bytes=64) for x in range(2)]
         ys = [sb.tile([P, HALF, F], F32, name="ys%d" % x, align_bytes=64) for x in range(2)]
-        ac = [sb.tile([P, 2, HALF, F], BF16, name="ac%d" % x, align_bytes=64) for x in range(2)]
+        ac = [sb.tile([P, 2, HALF, 2, F // 2], BF16, name="ac%d" % x, align_bytes=64) for x in range(2)]
 
         def mask_y(x, j, d, f):
             nc.vector.scalar_tensor_tensor(out=ys[x][:, j, f], in0=zy[x][:, j, f], scalar=0.0, in1=d[j][:, f], op0=ALU.is_gt, op1=ALU.mult)
@@ -175,13 +182,20 @@ def tile_graphnetlayer_pa_v_kernel(tc, h, ew1, eb1, ew2, eb2, z_lr, z_rl, grad_o
         def mask_x(x, j, d, f):
             nc.vector.scalar_tensor_tensor(out=xs[x][:, j, f], in0=zx[x][:, j, f], scalar=0.0, in1=d[j + 1][:, f], op0=ALU.is_gt, op1=ALU.mult)
 
+        def by_u(t):
+            return t.rearrange("p (q u e) -> p u q e", u=2, e=2)
+
+        def ac_out(x, a, j, f):
+            return ac[x][:, a, j, :, f.start // 2 : f.stop // 2].rearrange("p u (q e) -> p u q e", e=2)
+
         def sums(x, lo, hi, f):
-            nc.vector.tensor_tensor(out=ac[x][:, 1, lo:hi, f], in0=xs[x][:, lo - 1 : hi - 1, f], in1=ys[x][:, lo:hi, f], op=ALU.add)
-            nc.vector.tensor_tensor(out=ac[x][:, 0, lo:hi, f], in0=xs[x][:, lo:hi, f], in1=ys[x][:, lo - 1 : hi - 1, f], op=ALU.add)
+            for j in range(lo, hi):
+                nc.vector.tensor_tensor(out=ac_out(x, 1, j, f), in0=by_u(xs[x][:, j - 1, f]), in1=by_u(ys[x][:, j, f]), op=ALU.add)
+                nc.vector.tensor_tensor(out=ac_out(x, 0, j, f), in0=by_u(xs[x][:, j, f]), in1=by_u(ys[x][:, j - 1, f]), op=ALU.add)
 
         def ends(x, f):
-            nc.scalar.copy(out=ac[x][:, 1, 0, f], in_=ys[x][:, 0, f])
-            nc.scalar.copy(out=ac[x][:, 0, 0, f], in_=xs[x][:, 0, f])
+            for a, t in ((1, ys), (0, xs)):
+                nc.gpsimd.tensor_scalar(out=ac_out(x, a, 0, f), in0=by_u(t[x][:, 0, f]), scalar1=1.0, scalar2=0.0, op0=ALU.mult, op1=ALU.add)
 
         ALL = slice(0, F)
         LO = slice(0, F // 2)
@@ -194,21 +208,22 @@ def tile_graphnetlayer_pa_v_kernel(tc, h, ew1, eb1, ew2, eb2, z_lr, z_rl, grad_o
         f_scl = [[sb.tile([P, 512], U8, name="f_scl%d%d" % (x, a), align_bytes=64) for a in range(2)] for x in range(2)]
 
         def token_tile():
-            t_grp = sb.tile([P, 2, F // 2, 4], BF16, name="t_grp", tag="t_grp", bufs=3, align_bytes=64)
+            t_grp = sb.tile([P, 2, 2, F // 4, 4], BF16, name="t_grp", tag="t_grp", bufs=3, align_bytes=64)
             return t_grp
 
         def token_group(t_grp, x, fh, a, eng):
-            copy(eng, t_grp[:, a].rearrange("p (c i) j -> p c j i", i=4), ac[x][:, a, :, FH[fh]].rearrange("p j (c i) -> p c j i", i=4))
+            src = ac[x][:, a, :, :, fh * (F // 4) : (fh + 1) * (F // 4)]
+            copy(eng, t_grp[:, :, a], src.rearrange("p j u c -> p u c j"))
 
         def token_quant(x, fh, t_grp):
-            quant(t_cod[x][fh][:], t_scl[x][fh][:], t_grp[:].rearrange("p a f j -> p (a f j)"), E5M2)
+            quant(t_cod[x][fh][:], t_scl[x][fh][:], t_grp[:].rearrange("p u a c j -> p (u a c j)"), E5M2)
 
         def feat_tile(x, a):
             f_grp = sb.tile([P, 512, 4], BF16, name="f_grp", tag="f_grp", bufs=2, align_bytes=64)
             return f_grp
 
-        def feat_bank(x, a, k, group):
-            return pair_transposes(ac[x][:, a, k, :], ac[x][:, a, 3 - k, :], group)
+        def feat_bank(x, a, k, i_bank, plain=0, mx=0):
+            return pair_transposes([[ac[x][:, a, s, u, :].bitcast(F32) for u in range(2)] for s in (k, 3 - k)], i_bank, plain, mx)
 
         def feat_copies(f_grp, k, b, engs):
             diag_copy(engs[0], b, EVEN0_ODD1, f_grp[:, tile_cols(k), :])
@@ -248,80 +263,82 @@ def tile_graphnetlayer_pa_v_kernel(tc, h, ew1, eb1, ew2, eb2, z_lr, z_rl, grad_o
 
         def out1_end(b, fh, m, eng):
             o = sb.tile([P, 2, F // 2], F32, name="o1", tag="o1", bufs=4, align_bytes=64)
-            copy(eng, o[:].rearrange("p a f -> p (a f)"), b[:])
+            copy(eng, o[:].rearrange("p a (q u e) -> p (a q) u e", u=2, e=2), b[:].rearrange("p (u n e) -> p n u e", u=2, e=2))
             nc.sync.dma_start(out=out1_view[:, m, :, FH[fh]], in_=o[:])
 
-        weight_bank(ew2_sb, 0, e_grp, 0, "S", "all")
-        weight_bank(ew2_sb, 2, e_grp, 1, "V", "all")
-        b0 = g_bank(0, 0, "all")
-        b1 = g_bank(0, 1, "all")
+        weight_bank(ew2_sb, 0, e_grp, 0, "S", 0, plain=4)
+        weight_bank(ew2_sb, 2, e_grp, 1, "V", 1, plain=1)
+        b0 = g_bank(0, 0, 2, plain=2)
+        b1 = g_bank(0, 1, 3, plain=1)
         g_copies(0, 0, b0, "VSS")
         g_copies(0, 1, b1, "SS")
         quant(e_cod[:], e_scl[:], flat(e_grp[:]), E4M3)
         g_quant(0, 0, 2)
-        d = [d_bank(0, 0)]
+        d = [d_bank(0, 0, 0, plain=2)]
         g_quant(0, 2, 4)
-        d.append(d_bank(0, 1))
-        g_quant(0, 4, 5)
+        d.append(d_bank(0, 1, 1))
         mask_y(0, 0, d, ALL)
-        d.append(d_bank(0, 2))
-        d.append(d_bank(0, 3))
-        d.append(d_bank(0, 4))
+        g_quant(0, 4, 5)
+        d.append(d_bank(0, 2, 2))
+        d.append(d_bank(0, 3, 3))
+        d.append(d_bank(0, 4, 4))
         mask_x(0, 0, d, ALL)
         ends(0, ALL)
         mask_y(0, 1, d, ALL)
         mask_x(0, 1, d, ALL)
+        b0 = g_bank(1, 0, 6)
+        b1 = g_bank(1, 1, 7, mx=1)
+        g_copies(1, 0, b0, "SSS")
+        g_copies(1, 1, b1, "SS")
+        warm(bank(5), 0, 3)
         sums(0, 1, 2, ALL)
         h_group(0, "S")
         mask_y(0, 2, d, ALL)
         mask_x(0, 2, d, ALL)
         sums(0, 2, 3, ALL)
         f0 = [feat_tile(0, 0), feat_tile(0, 1)]
-        h_group(1, "S")
         for a in range(2):
-            b = feat_bank(0, a, 1, "d")
+            b = feat_bank(0, a, 1, 2 - a, mx=3 - 3 * a)
             feat_copies(f0[a], 1, b, "SS")
+        weight_bank(ew1_sb, 0, w_grp[0], 0, "S", 5, mx=1)
+        weight_bank(ew1_sb, 2, w_grp[0], 1, "S", 6, mx=1)
         mask_y(0, 3, d, ALL)
         mask_x(0, 3, d, ALL)
         sums(0, 3, 4, ALL)
         for a in range(2):
-            b = feat_bank(0, a, 0, "d")
+            b = feat_bank(0, a, 0, 3 - 3 * a, mx=1 - a)
             feat_copies(f0[a], 0, b, "SS")
         t0 = token_tile()
         t1 = token_tile()
         token_group(t0, 0, 0, 1, "V")
-        token_group(t0, 0, 0, 0, "V")
-        b0 = g_bank(1, 0, "d")
-        b1 = g_bank(1, 1, "d")
-        g_copies(1, 0, b0, "SSS")
-        g_copies(1, 1, b1, "SS")
-        weight_bank(ew1_sb, 0, w_grp[0], 0, "S", "w")
-        weight_bank(ew1_sb, 2, w_grp[0], 1, "S", "w")
-        weight_bank(ew1_sb, 4, w_grp[1], 0, "S", "w")
-        feat_quant(0, 0, f0[0])
-        feat_quant(0, 1, f0[1])
-        token_quant(0, 0, t0)
         g_quant(1, 0, 2)
         g_quant(1, 2, 4)
         g_quant(1, 4, 5)
-        d = [d_bank(1, s) for s in range(5)]
-        weight_bank(ew1_sb, 6, w_grp[1], 1, "S", "w")
+        token_group(t0, 0, 0, 0, "V")
+        d = [d_bank(1, s, (4, 1, 2)[s]) for s in range(3)]
+        weight_bank(ew1_sb, 4, w_grp[1], 0, "S", 7)
+        d += [d_bank(1, s, (3, 0)[s - 3]) for s in range(3, 5)]
+        weight_bank(ew1_sb, 6, w_grp[1], 1, "S", 5)
+        feat_quant(0, 0, f0[0])
+        feat_quant(0, 1, f0[1])
+        token_quant(0, 0, t0)
+        h_group(1, "S")
         mask_y(1, 0, d, LO)
         mask_x(1, 0, d, LO)
         ends(1, LO)
+        quant(w_cod[0][:], w_scl[0][:], flat(w_grp[0][:]), E4M3)
+        quant(w_cod[1][:], w_scl[1][:], flat(w_grp[1][:]), E4M3)
+        for m in range(4):
+            b = bank((6, 7, 5, 6)[m])
+            out0_mx(b, 0, m, 0)
+            out0_mx(b, 0, m, 1)
+            out0_end(b, 0, m, "S")
         token_group(t1, 0, 1, 0, "S")
         token_group(t1, 0, 1, 1, "S")
         mask_y(1, 1, d, LO)
         mask_x(1, 1, d, LO)
-        quant(w_cod[0][:], w_scl[0][:], flat(w_grp[0][:]), E4M3)
         mask_y(1, 2, d, LO)
         mask_x(1, 2, d, LO)
-        quant(w_cod[1][:], w_scl[1][:], flat(w_grp[1][:]), E4M3)
-        for m in range(4):
-            b = bank("w")
-            out0_mx(b, 0, m, 0)
-            out0_mx(b, 0, m, 1)
-            out0_end(b, 0, m, "S")
         mask_y(1, 3, d, LO)
         mask_x(1, 3, d, LO)
         h_quant(0)
@@ -335,22 +352,32 @@ def tile_graphnetlayer_pa_v_kernel(tc, h, ew1, eb1, ew2, eb2, z_lr, z_rl, grad_o
         ends(1, HI)
         mask_y(1, 1, d, HI)
         mask_x(1, 1, d, HI)
+        token_quant(0, 1, t1)
         token_quant(1, 0, t0)
-        for m in range(4):
-            b = bank("w")
-            out1_mx(b, 0, m, 0)
-            out1_mx(b, 0, m, 1)
-            out1_end(b, 0, m, "S")
+        bt = [bank((7, 5, 6, 7)[m]) for m in range(3)]
+        for m in range(3):
+            out1_mx(bt[m], 0, m, 0)
+        warm(bank(4), 0, 2)
+        warm(bank(1), 0, 2)
+        for m in range(3):
+            out1_mx(bt[m], 0, m, 1)
+            out1_end(bt[m], 0, m, "S")
+        b = bank(7)
+        out1_mx(b, 0, 3, 0)
+        out1_mx(b, 0, 3, 1)
+        out1_end(b, 0, 3, "S")
         mask_y(1, 2, d, HI)
         mask_x(1, 2, d, HI)
         sums(1, 1, 3, HI)
         f1 = [feat_tile(1, 0), feat_tile(1, 1)]
         for a in range(2):
-            b = feat_bank(1, a, 1, "w")
+            b = feat_bank(1, a, 1, 5 + a)
             feat_copies(f1[a], 1, b, "SS")
+        bt = [bank((4, 1, 2, 3)[m]) for m in range(4)]
+        out1_mx(bt[0], 1, 0, 0)
+        out1_mx(bt[1], 1, 1, 0)
         mask_y(1, 3, d, HI)
         mask_x(1, 3, d, HI)
-        token_quant(0, 1, t1)
         sums(1, 3, 4, HI)
         t1 = token_tile()
         token_group(t1, 1, 1, 1, "V")
@@ -358,24 +385,23 @@ def tile_graphnetlayer_pa_v_kernel(tc, h, ew1, eb1, ew2, eb2, z_lr, z_rl, grad_o
         feat_quant(1, 1, f1[1], 2, 4)
         token_group(t1, 1, 1, 0, "V")
         for a in range(2):
-            b = feat_bank(1, a, 0, "w")
+            b = feat_bank(1, a, 0, 7 - 2 * a)
             feat_copies(f1[a], 0, b, "SS")
+        out1_mx(bt[2], 1, 2, 0)
+        out1_mx(bt[3], 1, 3, 0)
         bf = [None] * 4
         for m in (1, 2):
-            bf[m] = bank("all")
+            bf[m] = bank((0, 0, 6, 0)[m])
             out0_mx(bf[m], 1, m, 0)
             out0_mx(bf[m], 1, m, 1)
             out0_end(bf[m], 1, m, "S")
-        bt = [bank("all") for m in range(4)]
-        for m in range(4):
-            out1_mx(bt[m], 1, m, 0)
         token_quant(1, 1, t1)
         for m in range(4):
             out1_mx(bt[m], 1, m, 1)
         feat_quant(1, 0, f1[0], 0, 2)
         feat_quant(1, 1, f1[1], 0, 2)
         for m in (0, 3):
-            bf[m] = bank("all")
+            bf[m] = bank((7, 0, 0, 5)[m])
             out0_mx(bf[m], 1, m, 0)
             out0_mx(bf[m], 1, m, 1)
         for m in range(4):

@@ -12,399 +12,516 @@ E5M2 = mybir.dt.float8_e5m2_x4
 ALU = mybir.AluOpType
 
 P = 128
-CHAINS, NODES, H, F = 128, 8, 512, 512
-HALF = NODES // 2
-FLOPS = 2 * CHAINS * NODES * H * F * 5
-BYTES = 2 * (2 * 1024 * 512 + 1024 * 512 + 512 * 512) + 4 * 2 * 128 * 7 * 512 + 4 * 2 * 1024 * 512
+NODES = 8
+EDGES = NODES - 1
+SLOTS = 4
+H = 512
+F = 512
+TOKENS = P * NODES
 
-STORE = {0: 0, 3: 1, 1: 2, 2: 3, 4: 4}
+FLOPS = 5 * 2 * TOKENS * H * F
+BYTES = 2 * (2 * TOKENS * H + 2 * H * F + H * F) + 4 * 2 * P * EDGES * F + 4 * (TOKENS * H + 2 * H * F)
 
 
 def tile_graphnetlayer_pa_v_kernel(tc, h, ew1, eb1, ew2, eb2, z_lr, z_rl, grad_out, out_0, out_1):
     nc = tc.nc
+    SCALAR, VECTOR = nc.scalar, nc.vector
     with ExitStack() as ctx:
         sb = ctx.enter_context(tc.tile_pool(name="sb", bufs=1))
         ps = ctx.enter_context(tc.psum_pool(name="ps", bufs=1))
         ctx.enter_context(tc.manual_schedule())
 
-        def bank(i):
-            b = ps.tile([P, 512], F32, name="bank%d" % i)
+        def new_bank():
+            b = ps.tile([P, 512], F32, name="bank", tag="bank", bufs=8)
             return b
 
-        def copy(eng, out, in_):
-            if eng == "S":
-                nc.scalar.copy(out=out, in_=in_)
+        def copy(engine, out, in_):
+            if engine is SCALAR:
+                SCALAR.copy(out=out, in_=in_)
             else:
-                nc.vector.tensor_copy(out=out, in_=in_)
+                VECTOR.tensor_copy(out=out, in_=in_)
 
-        def quant(codes, scales, grouped, fmt):
+        def quantise(codes, scales, grouped, fmt):
             nc.vector.quantize_mx(out=codes.bitcast(fmt), scales=scales, in_=grouped)
 
-        zz = sb.tile([P, 512], BF16, name="zz", align_bytes=64)
-        nc.vector.memset(zz[:], 0.0)
-
-        def warm(b, plain, mx):
-            for i in range(plain):
-                nc.tensor.matmul(out=b[:], lhsT=zz[:, 0:P], rhs=zz[:], start=True, stop=True)
-            for i in range(mx):
-                nc.tensor.matmul_mx(out=b[:], lhsT=g_cod[0][:, 0:P].bitcast(E5M2), lhsT_scale=g_scl[0][:, 0:P],
-                                    rhs=e_cod[:].bitcast(E4M3), rhs_scale=e_scl[:], start=True, stop=True)
-
-        def flat(t):
+        def merge(t):
             return t.rearrange("q n t -> q (n t)")
 
         ew2_sb = sb.tile([P, 4, H], BF16, name="ew2_sb", align_bytes=64)
         ew1_sb = sb.tile([P, 8, F], BF16, name="ew1_sb", align_bytes=64)
-        h_sb = sb.tile([P, 2, HALF, H], BF16, name="h_sb", align_bytes=64)
-        g_sb = [sb.tile([P, HALF, H], BF16, name="g_sb%d" % x, align_bytes=64) for x in range(2)]
-        zx = [sb.tile([P, HALF, F], F32, name="zx%d" % x, align_bytes=64) for x in range(2)]
-        zy = [sb.tile([P, HALF, F], F32, name="zy%d" % x, align_bytes=64) for x in range(2)]
-
-        g_view = grad_out.rearrange("(x c) (n t) h -> x (c n) t h", x=2, n=2)
-        h_view = h.rearrange("(x c) n h -> c x n h", x=2)
-        lr_view = z_lr.rearrange("(x c) e f -> x c e f", x=2)
-        rl_view = z_rl.rearrange("(x c) e f -> x c e f", x=2)
+        h_sb = sb.tile([P, 2, SLOTS, H], BF16, name="h_sb", align_bytes=64)
+        grad_sb = sb.tile([P, NODES, H], BF16, name="grad_sb", align_bytes=64)
+        lr_sb = sb.tile([P, EDGES, F], F32, name="lr_sb", align_bytes=64)
+        rl_sb = sb.tile([P, EDGES, F], F32, name="rl_sb", align_bytes=64)
         ew2_view = ew2.rearrange("(i p) h -> p i h", p=P)
         ew1_view = ew1.rearrange("(i p) f -> p i f", p=P)
+        h_view = h.rearrange("(x c) (n t) h -> x (c n) t h", x=2, n=2)
 
-        def load(out, in_):
+        def dma(out, in_):
             nc.sync.dma_start(out=out, in_=in_)
 
-        def load_g(x):
-            load(g_sb[x][:, 0::3, :], g_view[x][:, 0::3, :])
-            load(g_sb[x][:, 1:3, :], g_view[x][:, 1:3, :])
+        def load_ew2(i):
+            dma(ew2_sb[:, i : i + 2, :], ew2_view[:, i : i + 2, :])
 
-        def load_z(x, j):
-            load(zy[x][1::2, j, :], lr_view[x][:, 6 - j, :])
-            if j % 2 == 0:
-                load(zy[x][0::2, j : j + 2, :], rl_view[x][:, j : j + 2, :])
-            load(zx[x][1::2, j, :], rl_view[x][:, 6 - j, :])
-            if j % 2 == 0:
-                load(zx[x][0::2, j : j + 2, :], lr_view[x][:, j : j + 2, :])
+        def load_ew1(a):
+            dma(ew1_sb[:, 4 * a : 4 * a + 4, :], ew1_view[:, 4 * a : 4 * a + 4, :])
+
+        def load_grad(n):
+            dma(grad_sb[:, n : n + 2, :], grad_out[:, n : n + 2, :])
+
+        def load_lr(e):
+            dma(lr_sb[:, e, :], z_lr[:, e, :])
+
+        def load_rl(e):
+            dma(rl_sb[:, e, :], z_rl[:, e, :])
 
         def load_h(x):
-            load(h_sb[0::2, x], h_view[:, x, 0:4, :])
-            for j in range(4):
-                load(h_sb[1::2, x, j, :], h_view[:, x, 7 - j, :])
+            dma(h_sb[:, x], h_view[x])
 
-        load(ew2_sb[:, 0:2, :], ew2_view[:, 0:2, :])
-        load(ew2_sb[:, 2:4, :], ew2_view[:, 2:4, :])
-        load_g(0)
-        load_z(0, 0)
-        load_z(0, 1)
-        load_g(1)
-        load_z(0, 2)
-        load_h(0)
-        load_z(0, 3)
-        load(ew1_sb[:, 0:4, :], ew1_view[:, 0:4, :])
-        load(ew1_sb[:, 4:8, :], ew1_view[:, 4:8, :])
-        load_h(1)
-        load_z(1, 0)
-        load_z(1, 1)
-        load_z(1, 2)
-        load_z(1, 3)
-
+        zeros = sb.tile([P, 512], BF16, name="zeros", align_bytes=64)
+        nc.vector.memset(zeros[:], 0.0)
         ident = sb.tile([P, P], F32, name="ident", align_bytes=64)
-        perm = sb.tile([P, P], F32, name="perm", align_bytes=64)
         make_identity(nc, ident[:])
-        nc.vector.tensor_copy(out=perm[:].rearrange("p (n c) -> p n c", n=2), in_=ident[:].rearrange("p (c n) -> p n c", n=2))
 
-        e_grp = sb.tile([P, 512, 4], BF16, name="e_grp", align_bytes=64)
-        e_cod = sb.tile([P, 512], U32, name="e_cod", align_bytes=64)
-        e_scl = sb.tile([P, 512], U8, name="e_scl", align_bytes=64)
-        w_grp = [sb.tile([P, 512, 4], BF16, name="w_grp%d" % a, align_bytes=64) for a in range(2)]
-        w_cod = [sb.tile([P, 512], U32, name="w_cod%d" % a, align_bytes=64) for a in range(2)]
-        w_scl = [sb.tile([P, 512], U8, name="w_scl%d" % a, align_bytes=64) for a in range(2)]
+        ew2_grp = sb.tile([P, F, 4], BF16, name="ew2_grp", align_bytes=64)
+        ew2_cod = sb.tile([P, F], U32, name="ew2_cod", align_bytes=64)
+        ew2_scl = sb.tile([P, F], U8, name="ew2_scl", align_bytes=64)
+        ew1_grp = [sb.tile([P, H, 4], BF16, name="ew1_grp%d" % a, align_bytes=64) for a in range(2)]
+        ew1_cod = [sb.tile([P, H], U32, name="ew1_cod%d" % a, align_bytes=64) for a in range(2)]
+        ew1_scl = [sb.tile([P, H], U8, name="ew1_scl%d" % a, align_bytes=64) for a in range(2)]
+        grad_grp = sb.tile([P, TOKENS, 4], BF16, name="grad_grp", align_bytes=64)
+        grad_cod = sb.tile([P, TOKENS], U32, name="grad_cod", align_bytes=64)
+        grad_scl = sb.tile([P, TOKENS], U8, name="grad_scl", align_bytes=64)
 
-        def weight_bank(src, i, grp, r, eng, i_bank, plain=0, mx=0):
-            b = bank(i_bank)
-            warm(b, plain, mx)
+        banks = {}
+
+        def keep_busy(n):
+            b = new_bank()
+            for i in range(n):
+                nc.tensor.matmul(out=b[:], lhsT=zeros[:, 0:P], rhs=zeros[:], start=True, stop=True)
+
+        def keep_busy_mx():
+            b = new_bank()
+            nc.tensor.matmul_mx(
+                out=b[:],
+                lhsT=grad_cod[:, 0:P].bitcast(E5M2),
+                lhsT_scale=grad_scl[:, 0:P],
+                rhs=ew2_cod[:].bitcast(E4M3),
+                rhs_scale=ew2_scl[:],
+                start=True,
+                stop=True,
+            )
+
+        def turn_rows(key, rows):
+            b = banks[key] = new_bank()
             for d in range(2):
-                words = src[:, i + d, :].bitcast(F32)
+                words = rows[d].bitcast(F32)
                 for u in range(2):
-                    nc.tensor.transpose(b[:, d * 256 + u * 128 : d * 256 + u * 128 + 128], words[:, u::2], ident[:])
-            dst = flat(grp[:]).bitcast(F32)[:, r * 512 : (r + 1) * 512]
-            copy(eng, dst.rearrange("q (d p u) -> q d p u", d=2, u=2), b[:].rearrange("q (d u p) -> q d p u", d=2, u=2))
+                    nc.tensor.transpose(b[:, d * 256 + u * P : d * 256 + (u + 1) * P], words[:, u::2], ident[:])
 
-        g_grp = [sb.tile([P, 5 * P, 4], BF16, name="g_grp%d" % x, align_bytes=64) for x in range(2)]
-        g_cod = [sb.tile([P, 5 * P], U32, name="g_cod%d" % x, align_bytes=64) for x in range(2)]
-        g_scl = [sb.tile([P, 5 * P], U8, name="g_scl%d" % x, align_bytes=64) for x in range(2)]
+        def gather_rows(key, grp, r, engine):
+            dst = merge(grp[:]).bitcast(F32)[:, r * 512 : (r + 1) * 512]
+            src = banks[key][:].rearrange("q (d u p) -> q d p u", d=2, u=2)
+            copy(engine, dst.rearrange("q (d p u) -> q d p u", d=2, u=2), src)
 
-        def pair_transposes(words, i_bank, plain=0, mx=0):
-            b = bank(i_bank)
-            warm(b, plain, mx)
-            for k in range(2):
-                for u in range(2):
-                    nc.tensor.transpose(b[:, u * 256 + k * 128 : u * 256 + k * 128 + 128], words[k][u], perm[:])
-            return b
+        def turn_ew2(i):
+            turn_rows(("ew2", i), (ew2_sb[:, i, :], ew2_sb[:, i + 1, :]))
 
-        EVEN0_ODD1 = slice(0, 4, 3)
-        EVEN1_ODD0 = slice(2, 0, -1)
-        ODD0_EVEN1 = slice(1, 3)
+        def gather_ew2(i, engine):
+            gather_rows(("ew2", i), ew2_grp, i // 2, engine)
 
-        def diag_copy(eng, b, sel, dst_cols):
-            src_v = b[:].rearrange("q (u m c) -> q u m c", u=2, m=4)[:, :, sel, :].rearrange("q u n c -> q c n u")
-            dst_v = flat(dst_cols).bitcast(F32).rearrange("q (c n u) -> q c n u", n=2, u=2)
-            copy(eng, dst_v, src_v)
+        def quantise_ew2():
+            quantise(ew2_cod[:], ew2_scl[:], merge(ew2_grp[:]), E4M3)
 
-        def tile_cols(slot):
-            s = STORE[slot]
-            return slice(s * P, (s + 1) * P)
+        def turn_ew1(a, i):
+            turn_rows(("ew1", a, i), (ew1_sb[:, 4 * a + i, :], ew1_sb[:, 4 * a + i + 1, :]))
 
-        def g_bank(x, k, i_bank, plain=0, mx=0):
-            return pair_transposes([[g_sb[x][:, s, :].bitcast(F32)[:, u::2] for u in range(2)] for s in (k, 3 - k)], i_bank, plain, mx)
+        def gather_ew1(a, i, engine):
+            gather_rows(("ew1", a, i), ew1_grp[a], i // 2, engine)
 
-        def g_copies(x, k, b, engs):
-            diag_copy(engs[0], b, EVEN0_ODD1, g_grp[x][:, tile_cols(k), :])
-            diag_copy(engs[1], b, EVEN1_ODD0, g_grp[x][:, tile_cols(3 - k), :])
-            if k == 0:
-                diag_copy(engs[2], b, ODD0_EVEN1, g_grp[x][:, tile_cols(4), :])
+        def quantise_ew1(a):
+            quantise(ew1_cod[a][:], ew1_scl[a][:], merge(ew1_grp[a][:]), E4M3)
 
-        def g_quant(x, lo, hi):
-            c = slice(lo * P, hi * P)
-            quant(g_cod[x][:, c], g_scl[x][:, c], flat(g_grp[x][:, c, :]), E5M2)
+        def turn_grad(n):
+            turn_rows(("grad", n), (grad_sb[:, n, :], grad_sb[:, n + 1, :]))
 
-        def d_bank(x, slot, i_bank, plain=0, mx=0):
-            b = bank(i_bank)
-            warm(b, plain, mx)
-            c = tile_cols(slot)
-            nc.tensor.matmul_mx(out=b[:], lhsT=g_cod[x][:, c].bitcast(E5M2), lhsT_scale=g_scl[x][:, c],
-                                rhs=e_cod[:].bitcast(E4M3), rhs_scale=e_scl[:], start=True, stop=True)
-            return b
+        def gather_grad(n, engine):
+            gather_rows(("grad", n), grad_grp, n // 2, engine)
 
-        xs = [sb.tile([P, HALF, F], F32, name="xs%d" % x, align_bytes=64) for x in range(2)]
-        ys = [sb.tile([P, HALF, F], F32, name="ys%d" % x, align_bytes=64) for x in range(2)]
-        ac = [sb.tile([P, 2, HALF, 2, F // 2], BF16, name="ac%d" % x, align_bytes=64) for x in range(2)]
+        def quantise_grad(n):
+            c = slice(n * P, (n + 2) * P)
+            quantise(grad_cod[:, c], grad_scl[:, c], merge(grad_grp[:, c, :]), E5M2)
 
-        def mask_y(x, j, d, f):
-            nc.vector.scalar_tensor_tensor(out=ys[x][:, j, f], in0=zy[x][:, j, f], scalar=0.0, in1=d[j][:, f], op0=ALU.is_gt, op1=ALU.mult)
+        def product_d(n):
+            b = banks["d", n] = new_bank()
+            c = slice(n * P, (n + 1) * P)
+            nc.tensor.matmul_mx(
+                out=b[:],
+                lhsT=grad_cod[:, c].bitcast(E5M2),
+                lhsT_scale=grad_scl[:, c],
+                rhs=ew2_cod[:].bitcast(E4M3),
+                rhs_scale=ew2_scl[:],
+                start=True,
+                stop=True,
+            )
 
-        def mask_x(x, j, d, f):
-            nc.vector.scalar_tensor_tensor(out=xs[x][:, j, f], in0=zx[x][:, j, f], scalar=0.0, in1=d[j + 1][:, f], op0=ALU.is_gt, op1=ALU.mult)
+        to_right = sb.tile([P, EDGES, F], F32, name="to_right", align_bytes=64)
+        to_left = sb.tile([P, EDGES, F], F32, name="to_left", align_bytes=64)
+        dz = [sb.tile([P, NODES, 2, F // 2], BF16, name="dz%d" % a, align_bytes=64) for a in range(2)]
+
+        def masked(dst, z, d):
+            nc.vector.scalar_tensor_tensor(out=dst, in0=z, scalar=0.0, in1=d, op0=ALU.is_gt, op1=ALU.mult)
+
+        def mask_lr(n):
+            masked(to_right[:, n - 1, :], lr_sb[:, n - 1, :], banks["d", n][:])
+
+        def mask_rl(n):
+            masked(to_left[:, n, :], rl_sb[:, n, :], banks["d", n][:])
 
         def by_u(t):
             return t.rearrange("p (q u e) -> p u q e", u=2, e=2)
 
-        def ac_out(x, a, j, f):
-            return ac[x][:, a, j, :, f.start // 2 : f.stop // 2].rearrange("p u (q e) -> p u q e", e=2)
+        def dz_node(a, n):
+            return dz[a][:, n, :, :].rearrange("p u (q e) -> p u q e", e=2)
 
-        def sums(x, lo, hi, f):
-            for j in range(lo, hi):
-                nc.vector.tensor_tensor(out=ac_out(x, 1, j, f), in0=by_u(xs[x][:, j - 1, f]), in1=by_u(ys[x][:, j, f]), op=ALU.add)
-                nc.vector.tensor_tensor(out=ac_out(x, 0, j, f), in0=by_u(xs[x][:, j, f]), in1=by_u(ys[x][:, j - 1, f]), op=ALU.add)
+        def sum_a(n):
+            nc.vector.tensor_tensor(
+                out=dz_node(0, n), in0=by_u(to_right[:, n, :]), in1=by_u(to_left[:, n - 1, :]), op=ALU.add
+            )
 
-        def ends(x, f):
-            for a, t in ((1, ys), (0, xs)):
-                nc.gpsimd.tensor_scalar(out=ac_out(x, a, 0, f), in0=by_u(t[x][:, 0, f]), scalar1=1.0, scalar2=0.0, op0=ALU.mult, op1=ALU.add)
+        def sum_c(n):
+            nc.vector.tensor_tensor(
+                out=dz_node(1, n), in0=by_u(to_right[:, n - 1, :]), in1=by_u(to_left[:, n, :]), op=ALU.add
+            )
 
-        ALL = slice(0, F)
-        LO = slice(0, F // 2)
-        HI = slice(F // 2, F)
-        FH = (LO, HI)
+        end_terms = {
+            (0, 0): to_right[:, 0, :],
+            (1, 0): to_left[:, 0, :],
+            (0, NODES - 1): to_left[:, EDGES - 1, :],
+            (1, NODES - 1): to_right[:, EDGES - 1, :],
+        }
 
-        t_cod = [[sb.tile([P, 512], U32, name="t_cod%d%d" % (x, a), align_bytes=64) for a in range(2)] for x in range(2)]
-        t_scl = [[sb.tile([P, 512], U8, name="t_scl%d%d" % (x, a), align_bytes=64) for a in range(2)] for x in range(2)]
-        f_cod = [[sb.tile([P, 512], U32, name="f_cod%d%d" % (x, a), align_bytes=64) for a in range(2)] for x in range(2)]
-        f_scl = [[sb.tile([P, 512], U8, name="f_scl%d%d" % (x, a), align_bytes=64) for a in range(2)] for x in range(2)]
+        def end_node(a, n):
+            nc.gpsimd.tensor_scalar(
+                out=dz_node(a, n), in0=by_u(end_terms[a, n]), scalar1=1.0, scalar2=0.0, op0=ALU.mult, op1=ALU.add
+            )
 
-        def token_tile():
-            t_grp = sb.tile([P, 2, 2, F // 4, 4], BF16, name="t_grp", tag="t_grp", bufs=3, align_bytes=64)
-            return t_grp
+        f_grp = [sb.tile([P, SLOTS, 2 * P, 4], BF16, name="f_grp%d" % a, align_bytes=64) for a in range(2)]
+        f_cod = [sb.tile([P, TOKENS], U32, name="f_cod%d" % a, align_bytes=64) for a in range(2)]
+        f_scl = [sb.tile([P, TOKENS], U8, name="f_scl%d" % a, align_bytes=64) for a in range(2)]
+        t_cod = [[sb.tile([P, F], U32, name="t_cod%d%d" % (a, x), align_bytes=64) for x in range(2)] for a in range(2)]
+        t_scl = [[sb.tile([P, F], U8, name="t_scl%d%d" % (a, x), align_bytes=64) for x in range(2)] for a in range(2)]
 
-        def token_group(t_grp, x, fh, a, eng):
-            src = ac[x][:, a, :, :, fh * (F // 4) : (fh + 1) * (F // 4)]
-            copy(eng, t_grp[:, :, a], src.rearrange("p j u c -> p u c j"))
+        def filling(key):
+            if key not in banks:
+                banks[key] = new_bank()
+            return banks[key]
 
-        def token_quant(x, fh, t_grp):
-            quant(t_cod[x][fh][:], t_scl[x][fh][:], t_grp[:].rearrange("p u a c j -> p (u a c j)"), E5M2)
+        def turn_dz(a, t, n2):
+            b = filling(("f", a, t))
+            for u in range(2):
+                c = n2 * 256 + u * P
+                nc.tensor.transpose(b[:, c : c + P], dz[a][:, t + SLOTS * n2, u, :].bitcast(F32), ident[:])
 
-        def feat_tile(x, a):
-            f_grp = sb.tile([P, 512, 4], BF16, name="f_grp", tag="f_grp", bufs=2, align_bytes=64)
-            return f_grp
+        def gather_dz(a, t, engine):
+            dst = merge(f_grp[a][:, t]).bitcast(F32).rearrange("q (c n u) -> q c n u", n=2, u=2)
+            copy(engine, dst, banks["f", a, t][:].rearrange("q (n u c) -> q c n u", n=2, u=2))
 
-        def feat_bank(x, a, k, i_bank, plain=0, mx=0):
-            return pair_transposes([[ac[x][:, a, s, u, :].bitcast(F32) for u in range(2)] for s in (k, 3 - k)], i_bank, plain, mx)
+        def quantise_features(a, t):
+            c = slice(t * 2 * P, (t + 1) * 2 * P)
+            quantise(f_cod[a][:, c], f_scl[a][:, c], merge(f_grp[a][:, t]), E5M2)
 
-        def feat_copies(f_grp, k, b, engs):
-            diag_copy(engs[0], b, EVEN0_ODD1, f_grp[:, tile_cols(k), :])
-            diag_copy(engs[1], b, EVEN1_ODD0, f_grp[:, tile_cols(3 - k), :])
+        t_grp = [
+            [sb.tile([P, 2, F // 2, SLOTS], BF16, name="t_grp%d%d" % (a, x), align_bytes=64) for x in range(2)]
+            for a in range(2)
+        ]
 
-        def feat_quant(x, a, f_grp, lo=0, hi=4):
-            c = slice(lo * P, hi * P)
-            quant(f_cod[x][a][:, c], f_scl[x][a][:, c], flat(f_grp[:, c, :]), E5M2)
+        def turn_back(a, x, u, t):
+            words = merge(f_grp[a][:, t, x * P : (x + 1) * P, :]).bitcast(F32)
+            b = filling(("t", a, x, u))
+            nc.tensor.transpose(b[:, t * P : (t + 1) * P], words[:, u::2], ident[:])
 
-        h_grp = [sb.tile([P, 512, 4], BF16, name="h_grp%d" % x, align_bytes=64) for x in range(2)]
-        h_cod = [sb.tile([P, 512], U32, name="h_cod%d" % x, align_bytes=64) for x in range(2)]
-        h_scl = [sb.tile([P, 512], U8, name="h_scl%d" % x, align_bytes=64) for x in range(2)]
+        def gather_tokens(a, x, u, engine):
+            copy(engine, t_grp[a][x][:, u], banks["t", a, x, u][:].bitcast(BF16).rearrange("p (t n) -> p n t", t=SLOTS))
 
-        def h_group(x, eng):
-            copy(eng, h_grp[x][:].rearrange("p (c i) j -> p c j i", i=4), h_sb[:, x, :, :].rearrange("p j (c i) -> p c j i", i=4))
+        def quantise_tokens(a, x):
+            quantise(t_cod[a][x][:], t_scl[a][x][:], t_grp[a][x][:].rearrange("p u n t -> p (u n t)"), E5M2)
 
-        def h_quant(x):
-            quant(h_cod[x][:], h_scl[x][:], flat(h_grp[x][:]), E4M3)
+        h_grp = [sb.tile([P, H, SLOTS], BF16, name="h_grp%d" % x, align_bytes=64) for x in range(2)]
+        h_cod = [sb.tile([P, H], U32, name="h_cod%d" % x, align_bytes=64) for x in range(2)]
+        h_scl = [sb.tile([P, H], U8, name="h_scl%d" % x, align_bytes=64) for x in range(2)]
 
-        out0_view = out_0.rearrange("(x c) (n m) h -> x (c n) m h", x=2, n=2)
-        out1_view = out_1.rearrange("(a m p) f -> p m a f", a=2, p=P)
-        o0 = [sb.tile([P, 4, H], F32, name="o0_%d" % x, align_bytes=64) for x in range(2)]
+        def gather_h(x, i, engine):
+            c = slice(i * P, (i + 1) * P)
+            dst = h_grp[x][:, c, :].rearrange("p (c i) t -> p c t i", i=4)
+            copy(engine, dst, h_sb[:, x, :, c].rearrange("p t (c i) -> p c t i", i=4))
 
-        def out0_mx(b, x, m, a):
-            c = tile_cols(m)
-            nc.tensor.matmul_mx(out=b[:], lhsT=f_cod[x][a][:, c].bitcast(E5M2), lhsT_scale=f_scl[x][a][:, c],
-                                rhs=w_cod[a][:].bitcast(E4M3), rhs_scale=w_scl[a][:], start=(a == 0), stop=(a == 1))
+        def quantise_h(x):
+            quantise(h_cod[x][:], h_scl[x][:], merge(h_grp[x][:]), E4M3)
 
-        def out0_end(b, x, m, eng):
-            copy(eng, o0[x][:, m, :], b[:])
-            nc.sync.dma_start(out=out0_view[x][:, m, :], in_=o0[x][:, m, :])
+        out0_view = out_0.rearrange("(x c) (n t) h -> x (c n) t h", x=2, n=2)
+        out1_view = out_1.rearrange("(a m p) f -> a p m f", a=2, p=P)
 
-        def out1_mx(b, fh, m, x):
+        def product_dx(t, x, a):
+            c = slice(t * 2 * P + x * P, t * 2 * P + (x + 1) * P)
+            nc.tensor.matmul_mx(
+                out=filling(("dx", t, x))[:],
+                lhsT=f_cod[a][:, c].bitcast(E5M2),
+                lhsT_scale=f_scl[a][:, c],
+                rhs=ew1_cod[a][:].bitcast(E4M3),
+                rhs_scale=ew1_scl[a][:],
+                start=(a == 0),
+                stop=(a == 1),
+            )
+
+        def store_dx(t, x, engine):
+            o = sb.tile([P, H], F32, name="dx_out", tag="dx_out", bufs=6, align_bytes=64)
+            copy(engine, o[:], banks["dx", t, x][:])
+            dma(out0_view[x][:, t, :], o[:])
+
+        def product_dw(a, m, x):
             c = slice(m * P, (m + 1) * P)
-            nc.tensor.matmul_mx(out=b[:], lhsT=h_cod[x][:, c].bitcast(E4M3), lhsT_scale=h_scl[x][:, c],
-                                rhs=t_cod[x][fh][:].bitcast(E5M2), rhs_scale=t_scl[x][fh][:], start=(x == 0), stop=(x == 1))
+            nc.tensor.matmul_mx(
+                out=filling(("dw", a, m))[:],
+                lhsT=h_cod[x][:, c].bitcast(E4M3),
+                lhsT_scale=h_scl[x][:, c],
+                rhs=t_cod[a][x][:].bitcast(E5M2),
+                rhs_scale=t_scl[a][x][:],
+                start=(x == 0),
+                stop=(x == 1),
+            )
 
-        def out1_end(b, fh, m, eng):
-            o = sb.tile([P, 2, F // 2], F32, name="o1", tag="o1", bufs=4, align_bytes=64)
-            copy(eng, o[:].rearrange("p a (q u e) -> p (a q) u e", u=2, e=2), b[:].rearrange("p (u n e) -> p n u e", u=2, e=2))
-            nc.sync.dma_start(out=out1_view[:, m, :, FH[fh]], in_=o[:])
+        def store_dw(a, m, engine):
+            o = sb.tile([P, F], F32, name="dw_out", tag="dw_out", bufs=6, align_bytes=64)
+            dst = o[:].rearrange("p (q u e) -> p q u e", u=2, e=2)
+            copy(engine, dst, banks["dw", a, m][:].rearrange("p (u q e) -> p q u e", u=2, e=2))
+            dma(out1_view[a][:, m, :], o[:])
 
-        weight_bank(ew2_sb, 0, e_grp, 0, "S", 0, plain=4)
-        weight_bank(ew2_sb, 2, e_grp, 1, "V", 1, plain=1)
-        b0 = g_bank(0, 0, 2, plain=2)
-        b1 = g_bank(0, 1, 3, plain=1)
-        g_copies(0, 0, b0, "VSS")
-        g_copies(0, 1, b1, "SS")
-        quant(e_cod[:], e_scl[:], flat(e_grp[:]), E4M3)
-        g_quant(0, 0, 2)
-        d = [d_bank(0, 0, 0, plain=2)]
-        g_quant(0, 2, 4)
-        d.append(d_bank(0, 1, 1))
-        mask_y(0, 0, d, ALL)
-        g_quant(0, 4, 5)
-        d.append(d_bank(0, 2, 2))
-        d.append(d_bank(0, 3, 3))
-        d.append(d_bank(0, 4, 4))
-        mask_x(0, 0, d, ALL)
-        ends(0, ALL)
-        mask_y(0, 1, d, ALL)
-        mask_x(0, 1, d, ALL)
-        b0 = g_bank(1, 0, 6)
-        b1 = g_bank(1, 1, 7, mx=1)
-        g_copies(1, 0, b0, "SSS")
-        g_copies(1, 1, b1, "SS")
-        warm(bank(5), 0, 3)
-        sums(0, 1, 2, ALL)
-        h_group(0, "S")
-        mask_y(0, 2, d, ALL)
-        mask_x(0, 2, d, ALL)
-        sums(0, 2, 3, ALL)
-        f0 = [feat_tile(0, 0), feat_tile(0, 1)]
-        for a in range(2):
-            b = feat_bank(0, a, 1, 2 - a, mx=3 - 3 * a)
-            feat_copies(f0[a], 1, b, "SS")
-        weight_bank(ew1_sb, 0, w_grp[0], 0, "S", 5, mx=1)
-        weight_bank(ew1_sb, 2, w_grp[0], 1, "S", 6, mx=1)
-        mask_y(0, 3, d, ALL)
-        mask_x(0, 3, d, ALL)
-        sums(0, 3, 4, ALL)
-        for a in range(2):
-            b = feat_bank(0, a, 0, 3 - 3 * a, mx=1 - a)
-            feat_copies(f0[a], 0, b, "SS")
-        t0 = token_tile()
-        t1 = token_tile()
-        token_group(t0, 0, 0, 1, "V")
-        g_quant(1, 0, 2)
-        g_quant(1, 2, 4)
-        g_quant(1, 4, 5)
-        token_group(t0, 0, 0, 0, "V")
-        d = [d_bank(1, s, (4, 1, 2)[s]) for s in range(3)]
-        weight_bank(ew1_sb, 4, w_grp[1], 0, "S", 7)
-        d += [d_bank(1, s, (3, 0)[s - 3]) for s in range(3, 5)]
-        weight_bank(ew1_sb, 6, w_grp[1], 1, "S", 5)
-        feat_quant(0, 0, f0[0])
-        feat_quant(0, 1, f0[1])
-        token_quant(0, 0, t0)
-        h_group(1, "S")
-        mask_y(1, 0, d, LO)
-        mask_x(1, 0, d, LO)
-        ends(1, LO)
-        quant(w_cod[0][:], w_scl[0][:], flat(w_grp[0][:]), E4M3)
-        quant(w_cod[1][:], w_scl[1][:], flat(w_grp[1][:]), E4M3)
-        for m in range(4):
-            b = bank((6, 7, 5, 6)[m])
-            out0_mx(b, 0, m, 0)
-            out0_mx(b, 0, m, 1)
-            out0_end(b, 0, m, "S")
-        token_group(t1, 0, 1, 0, "S")
-        token_group(t1, 0, 1, 1, "S")
-        mask_y(1, 1, d, LO)
-        mask_x(1, 1, d, LO)
-        mask_y(1, 2, d, LO)
-        mask_x(1, 2, d, LO)
-        mask_y(1, 3, d, LO)
-        mask_x(1, 3, d, LO)
-        h_quant(0)
-        sums(1, 1, 4, LO)
-        h_quant(1)
-        t0 = token_tile()
-        token_group(t0, 1, 0, 1, "S")
-        token_group(t0, 1, 0, 0, "V")
-        mask_y(1, 0, d, HI)
-        mask_x(1, 0, d, HI)
-        ends(1, HI)
-        mask_y(1, 1, d, HI)
-        mask_x(1, 1, d, HI)
-        token_quant(0, 1, t1)
-        token_quant(1, 0, t0)
-        bt = [bank((7, 5, 6, 7)[m]) for m in range(3)]
-        for m in range(3):
-            out1_mx(bt[m], 0, m, 0)
-        warm(bank(4), 0, 2)
-        warm(bank(1), 0, 2)
-        for m in range(3):
-            out1_mx(bt[m], 0, m, 1)
-            out1_end(bt[m], 0, m, "S")
-        b = bank(7)
-        out1_mx(b, 0, 3, 0)
-        out1_mx(b, 0, 3, 1)
-        out1_end(b, 0, 3, "S")
-        mask_y(1, 2, d, HI)
-        mask_x(1, 2, d, HI)
-        sums(1, 1, 3, HI)
-        f1 = [feat_tile(1, 0), feat_tile(1, 1)]
-        for a in range(2):
-            b = feat_bank(1, a, 1, 5 + a)
-            feat_copies(f1[a], 1, b, "SS")
-        bt = [bank((4, 1, 2, 3)[m]) for m in range(4)]
-        out1_mx(bt[0], 1, 0, 0)
-        out1_mx(bt[1], 1, 1, 0)
-        mask_y(1, 3, d, HI)
-        mask_x(1, 3, d, HI)
-        sums(1, 3, 4, HI)
-        t1 = token_tile()
-        token_group(t1, 1, 1, 1, "V")
-        feat_quant(1, 0, f1[0], 2, 4)
-        feat_quant(1, 1, f1[1], 2, 4)
-        token_group(t1, 1, 1, 0, "V")
-        for a in range(2):
-            b = feat_bank(1, a, 0, 7 - 2 * a)
-            feat_copies(f1[a], 0, b, "SS")
-        out1_mx(bt[2], 1, 2, 0)
-        out1_mx(bt[3], 1, 3, 0)
-        bf = [None] * 4
-        for m in (1, 2):
-            bf[m] = bank((0, 0, 6, 0)[m])
-            out0_mx(bf[m], 1, m, 0)
-            out0_mx(bf[m], 1, m, 1)
-            out0_end(bf[m], 1, m, "S")
-        token_quant(1, 1, t1)
-        for m in range(4):
-            out1_mx(bt[m], 1, m, 1)
-        feat_quant(1, 0, f1[0], 0, 2)
-        feat_quant(1, 1, f1[1], 0, 2)
-        for m in (0, 3):
-            bf[m] = bank((7, 0, 0, 5)[m])
-            out0_mx(bf[m], 1, m, 0)
-            out0_mx(bf[m], 1, m, 1)
-        for m in range(4):
-            out1_end(bt[m], 1, m, "SV"[m % 2])
-        out0_end(bf[0], 1, 0, "S")
-        out0_end(bf[3], 1, 3, "V")
+        load_ew2(0)
+        load_grad(4)
+        load_ew2(2)
+        load_grad(2)
+        load_grad(6)
+        load_grad(0)
+        load_lr(2)
+        load_lr(4)
+        turn_ew2(0)
+        load_rl(3)
+        load_rl(5)
+        turn_grad(4)
+        gather_ew2(0, SCALAR)
+        load_ew1(1)
+        turn_ew2(2)
+        gather_grad(4, SCALAR)
+        load_lr(0)
+        turn_grad(2)
+        gather_ew2(2, VECTOR)
+        load_lr(6)
+        turn_grad(6)
+        load_rl(1)
+        gather_grad(2, SCALAR)
+        quantise_ew2()
+        turn_grad(0)
+        load_h(0)
+        gather_grad(6, SCALAR)
+        quantise_grad(2)
+        quantise_grad(4)
+        product_d(3)
+        load_ew1(0)
+        gather_grad(0, SCALAR)
+        quantise_grad(6)
+        load_lr(1)
+        product_d(5)
+        quantise_grad(0)
+        mask_lr(3)
+        load_rl(0)
+        product_d(6)
+        mask_rl(3)
+        product_d(1)
+        mask_lr(5)
+        turn_ew1(1, 0)
+        load_rl(4)
+        mask_rl(5)
+        load_lr(3)
+        turn_ew1(1, 2)
+        gather_ew1(1, 0, SCALAR)
+        mask_lr(1)
+        load_h(1)
+        product_d(0)
+        gather_ew1(1, 2, SCALAR)
+        product_d(7)
+        sum_c(5)
+        end_node(0, 0)
+        load_rl(2)
+        product_d(2)
+        sum_c(3)
+        mask_rl(1)
+        turn_dz(1, 3, 0)
+        gather_h(0, 0, SCALAR)
+        load_lr(5)
+        product_d(4)
+        sum_a(4)
+        gather_h(0, 3, SCALAR)
+        sum_c(1)
+        turn_ew1(0, 2)
+        load_rl(6)
+        gather_h(0, 1, SCALAR)
+        sum_a(2)
+        turn_dz(0, 0, 0)
+        turn_dz(0, 0, 1)
+        mask_lr(7)
+        gather_ew1(0, 2, SCALAR)
+        mask_rl(0)
+        gather_h(0, 2, SCALAR)
+        turn_dz(1, 1, 0)
+        end_node(1, 7)
+        turn_dz(1, 1, 1)
+        turn_ew1(0, 0)
+        mask_rl(4)
+        gather_dz(0, 0, SCALAR)
+        sum_a(6)
+        keep_busy_mx()
+        gather_dz(1, 1, SCALAR)
+        mask_lr(2)
+        turn_dz(1, 3, 1)
+        gather_h(1, 0, SCALAR)
+        mask_lr(4)
+        turn_dz(0, 2, 0)
+        turn_back(0, 1, 1, 0)
+        turn_back(0, 0, 0, 0)
+        gather_dz(1, 3, SCALAR)
+        turn_dz(0, 2, 1)
+        mask_rl(2)
+        turn_back(1, 1, 1, 1)
+        gather_h(1, 1, SCALAR)
+        turn_back(1, 1, 1, 3)
+        mask_lr(6)
+        turn_back(0, 0, 1, 0)
+        keep_busy(4)
+        gather_h(1, 2, SCALAR)
+        mask_rl(6)
+        sum_a(1)
+        gather_ew1(0, 0, SCALAR)
+        end_node(0, 7)
+        sum_a(3)
+        gather_dz(0, 2, SCALAR)
+        end_node(1, 0)
+        turn_dz(0, 1, 0)
+        sum_a(5)
+        gather_h(1, 3, SCALAR)
+        turn_dz(0, 3, 1)
+        turn_dz(0, 3, 0)
+        keep_busy(1)
+        sum_c(4)
+        turn_back(0, 0, 1, 2)
+        gather_dz(0, 3, SCALAR)
+        turn_dz(0, 1, 1)
+        turn_dz(1, 0, 0)
+        turn_back(0, 1, 0, 0)
+        sum_c(2)
+        turn_back(0, 0, 0, 2)
+        gather_dz(0, 1, SCALAR)
+        turn_dz(1, 0, 1)
+        turn_back(0, 0, 1, 3)
+        turn_back(0, 0, 0, 3)
+        sum_c(6)
+        turn_back(1, 0, 1, 3)
+        gather_dz(1, 0, SCALAR)
+        turn_back(0, 0, 0, 1)
+        keep_busy(2)
+        quantise_ew1(0)
+        gather_tokens(0, 0, 0, SCALAR)
+        turn_back(0, 1, 1, 2)
+        turn_dz(1, 2, 1)
+        turn_dz(1, 2, 0)
+        quantise_features(1, 3)
+        turn_back(0, 1, 0, 3)
+        turn_back(0, 1, 1, 1)
+        quantise_features(0, 3)
+        turn_back(0, 1, 1, 3)
+        gather_dz(1, 2, SCALAR)
+        turn_back(0, 0, 1, 1)
+        turn_back(1, 0, 1, 0)
+        quantise_features(0, 1)
+        turn_back(1, 0, 0, 0)
+        turn_back(1, 0, 0, 1)
+        quantise_features(0, 2)
+        gather_tokens(0, 0, 1, SCALAR)
+        turn_back(0, 1, 0, 2)
+        turn_back(0, 1, 0, 1)
+        turn_back(1, 0, 0, 3)
+        quantise_features(1, 1)
+        turn_back(1, 0, 0, 2)
+        turn_back(1, 1, 0, 3)
+        quantise_ew1(1)
+        turn_back(1, 1, 0, 1)
+        turn_back(1, 0, 1, 2)
+        gather_tokens(0, 1, 0, SCALAR)
+        product_dx(3, 1, 0)
+        quantise_h(0)
+        product_dx(3, 0, 0)
+        product_dx(3, 0, 1)
+        gather_tokens(0, 1, 1, SCALAR)
+        turn_back(1, 0, 1, 1)
+        quantise_h(1)
+        turn_back(1, 1, 0, 0)
+        turn_back(1, 1, 0, 2)
+        product_dx(3, 1, 1)
+        quantise_features(1, 2)
+        store_dx(3, 0, SCALAR)
+        product_dx(1, 1, 0)
+        quantise_tokens(0, 0)
+        product_dx(1, 0, 0)
+        store_dx(3, 1, SCALAR)
+        product_dx(1, 0, 1)
+        quantise_tokens(0, 1)
+        product_dx(1, 1, 1)
+        product_dw(0, 2, 0)
+        store_dx(1, 0, SCALAR)
+        gather_tokens(1, 0, 1, VECTOR)
+        product_dw(0, 2, 1)
+        product_dx(2, 0, 0)
+        store_dx(1, 1, SCALAR)
+        product_dx(2, 0, 1)
+        gather_tokens(1, 1, 0, VECTOR)
+        product_dw(0, 3, 0)
+        store_dw(0, 2, SCALAR)
+        product_dw(0, 3, 1)
+        product_dw(0, 0, 0)
+        store_dx(2, 0, SCALAR)
+        product_dw(0, 0, 1)
+        store_dw(0, 3, VECTOR)
+        product_dx(2, 1, 0)
+        gather_tokens(1, 0, 0, SCALAR)
+        turn_back(1, 1, 1, 0)
+        store_dw(0, 0, VECTOR)
+        turn_back(1, 1, 1, 2)
+        product_dx(2, 1, 1)
+        quantise_features(1, 0)
+        product_dw(0, 1, 0)
+        gather_tokens(1, 1, 1, SCALAR)
+        quantise_features(0, 0)
+        product_dw(0, 1, 1)
+        store_dx(2, 1, VECTOR)
+        product_dx(0, 1, 0)
+        store_dw(0, 1, SCALAR)
+        product_dx(0, 0, 0)
+        quantise_tokens(1, 0)
+        product_dx(0, 1, 1)
+        product_dx(0, 0, 1)
+        quantise_tokens(1, 1)
+        store_dx(0, 1, SCALAR)
+        product_dw(1, 1, 0)
+        product_dw(1, 2, 0)
+        store_dx(0, 0, VECTOR)
+        product_dw(1, 1, 1)
+        product_dw(1, 0, 0)
+        product_dw(1, 2, 1)
+        store_dw(1, 1, VECTOR)
+        product_dw(1, 0, 1)
+        keep_busy_mx()
+        store_dw(1, 2, VECTOR)
+        product_dw(1, 3, 0)
+        product_dw(1, 3, 1)
+        store_dw(1, 0, VECTOR)
+        store_dw(1, 3, SCALAR)

from contextlib import ExitStack

import concourse.mybir as mybir
from concourse.masks import make_identity

F32 = mybir.dt.float32
BF16 = mybir.dt.bfloat16
U32 = mybir.dt.uint32
U8 = mybir.dt.uint8
E4M3 = mybir.dt.float8_e4m3fn_x4
E5M2 = mybir.dt.float8_e5m2_x4
ALU = mybir.AluOpType

P = 128
NODES = 8
EDGES = NODES - 1
SLOTS = 4
H = 512
F = 512
TOKENS = P * NODES

FLOPS = 5 * 2 * TOKENS * H * F
BYTES = 2 * (2 * TOKENS * H + 2 * H * F + H * F) + 4 * 2 * P * EDGES * F + 4 * (TOKENS * H + 2 * H * F)


def tile_graphnetlayer_pa_v_kernel(tc, h, ew1, eb1, ew2, eb2, z_lr, z_rl, grad_out, out_0, out_1):
    nc = tc.nc
    SCALAR, VECTOR = nc.scalar, nc.vector
    with ExitStack() as ctx:
        sb = ctx.enter_context(tc.tile_pool(name="sb", bufs=1))
        ps = ctx.enter_context(tc.psum_pool(name="ps", bufs=1))
        ctx.enter_context(tc.manual_schedule())

        def new_bank():
            b = ps.tile([P, 512], F32, name="bank", tag="bank", bufs=8)
            return b

        def copy(engine, out, in_):
            if engine is SCALAR:
                SCALAR.copy(out=out, in_=in_)
            else:
                VECTOR.tensor_copy(out=out, in_=in_)

        def quantise(codes, scales, grouped, fmt):
            nc.vector.quantize_mx(out=codes.bitcast(fmt), scales=scales, in_=grouped)

        def merge(t):
            return t.rearrange("q n t -> q (n t)")

        ew2_sb = sb.tile([P, 4, H], BF16, name="ew2_sb", align_bytes=64)
        ew1_sb = sb.tile([P, 8, F], BF16, name="ew1_sb", align_bytes=64)
        h_sb = sb.tile([P, 2, SLOTS, H], BF16, name="h_sb", align_bytes=64)
        grad_sb = sb.tile([P, NODES, H], BF16, name="grad_sb", align_bytes=64)
        lr_sb = sb.tile([P, EDGES, F], F32, name="lr_sb", align_bytes=64)
        rl_sb = sb.tile([P, EDGES, F], F32, name="rl_sb", align_bytes=64)
        ew2_view = ew2.rearrange("(i p) h -> p i h", p=P)
        ew1_view = ew1.rearrange("(i p) f -> p i f", p=P)
        h_view = h.rearrange("(x c) (n t) h -> x (c n) t h", x=2, n=2)

        def dma(out, in_):
            nc.sync.dma_start(out=out, in_=in_)

        def load_ew2(i):
            dma(ew2_sb[:, i : i + 2, :], ew2_view[:, i : i + 2, :])

        def load_ew1(a):
            dma(ew1_sb[:, 4 * a : 4 * a + 4, :], ew1_view[:, 4 * a : 4 * a + 4, :])

        def load_grad(n):
            dma(grad_sb[:, n : n + 2, :], grad_out[:, n : n + 2, :])

        def load_lr(e):
            dma(lr_sb[:, e, :], z_lr[:, e, :])

        def load_rl(e):
            dma(rl_sb[:, e, :], z_rl[:, e, :])

        def load_h(x):
            dma(h_sb[:, x], h_view[x])

        zeros = sb.tile([P, 512], BF16, name="zeros", align_bytes=64)
        nc.vector.memset(zeros[:], 0.0)
        ident = sb.tile([P, P], F32, name="ident", align_bytes=64)
        make_identity(nc, ident[:])

        ew2_grp = sb.tile([P, F, 4], BF16, name="ew2_grp", align_bytes=64)
        ew2_cod = sb.tile([P, F], U32, name="ew2_cod", align_bytes=64)
        ew2_scl = sb.tile([P, F], U8, name="ew2_scl", align_bytes=64)
        ew1_grp = [sb.tile([P, H, 4], BF16, name="ew1_grp%d" % a, align_bytes=64) for a in range(2)]
        ew1_cod = [sb.tile([P, H], U32, name="ew1_cod%d" % a, align_bytes=64) for a in range(2)]
        ew1_scl = [sb.tile([P, H], U8, name="ew1_scl%d" % a, align_bytes=64) for a in range(2)]
        grad_grp = sb.tile([P, TOKENS, 4], BF16, name="grad_grp", align_bytes=64)
        grad_cod = sb.tile([P, TOKENS], U32, name="grad_cod", align_bytes=64)
        grad_scl = sb.tile([P, TOKENS], U8, name="grad_scl", align_bytes=64)

        banks = {}

        def keep_busy(n):
            b = new_bank()
            for i in range(n):
                nc.tensor.matmul(out=b[:], lhsT=zeros[:, 0:P], rhs=zeros[:], start=True, stop=True)

        def keep_busy_mx():
            b = new_bank()
            nc.tensor.matmul_mx(
                out=b[:],
                lhsT=grad_cod[:, 0:P].bitcast(E5M2),
                lhsT_scale=grad_scl[:, 0:P],
                rhs=ew2_cod[:].bitcast(E4M3),
                rhs_scale=ew2_scl[:],
                start=True,
                stop=True,
            )

        def turn_rows(key, rows):
            b = banks[key] = new_bank()
            for d in range(2):
                words = rows[d].bitcast(F32)
                for u in range(2):
                    nc.tensor.transpose(b[:, d * 256 + u * P : d * 256 + (u + 1) * P], words[:, u::2], ident[:])

        def gather_rows(key, grp, r, engine):
            dst = merge(grp[:]).bitcast(F32)[:, r * 512 : (r + 1) * 512]
            src = banks[key][:].rearrange("q (d u p) -> q d p u", d=2, u=2)
            copy(engine, dst.rearrange("q (d p u) -> q d p u", d=2, u=2), src)

        def turn_ew2(i):
            turn_rows(("ew2", i), (ew2_sb[:, i, :], ew2_sb[:, i + 1, :]))

        def gather_ew2(i, engine):
            gather_rows(("ew2", i), ew2_grp, i // 2, engine)

        def quantise_ew2():
            quantise(ew2_cod[:], ew2_scl[:], merge(ew2_grp[:]), E4M3)

        def turn_ew1(a, i):
            turn_rows(("ew1", a, i), (ew1_sb[:, 4 * a + i, :], ew1_sb[:, 4 * a + i + 1, :]))

        def gather_ew1(a, i, engine):
            gather_rows(("ew1", a, i), ew1_grp[a], i // 2, engine)

        def quantise_ew1(a):
            quantise(ew1_cod[a][:], ew1_scl[a][:], merge(ew1_grp[a][:]), E4M3)

        def turn_grad(n):
            turn_rows(("grad", n), (grad_sb[:, n, :], grad_sb[:, n + 1, :]))

        def gather_grad(n, engine):
            gather_rows(("grad", n), grad_grp, n // 2, engine)

        def quantise_grad(n):
            c = slice(n * P, (n + 2) * P)
            quantise(grad_cod[:, c], grad_scl[:, c], merge(grad_grp[:, c, :]), E5M2)

        def product_d(n):
            b = banks["d", n] = new_bank()
            c = slice(n * P, (n + 1) * P)
            nc.tensor.matmul_mx(
                out=b[:],
                lhsT=grad_cod[:, c].bitcast(E5M2),
                lhsT_scale=grad_scl[:, c],
                rhs=ew2_cod[:].bitcast(E4M3),
                rhs_scale=ew2_scl[:],
                start=True,
                stop=True,
            )

        to_right = sb.tile([P, EDGES, F], F32, name="to_right", align_bytes=64)
        to_left = sb.tile([P, EDGES, F], F32, name="to_left", align_bytes=64)
        dz = [sb.tile([P, NODES, 2, F // 2], BF16, name="dz%d" % a, align_bytes=64) for a in range(2)]

        def masked(dst, z, d):
            nc.vector.scalar_tensor_tensor(out=dst, in0=z, scalar=0.0, in1=d, op0=ALU.is_gt, op1=ALU.mult)

        def mask_lr(n):
            masked(to_right[:, n - 1, :], lr_sb[:, n - 1, :], banks["d", n][:])

        def mask_rl(n):
            masked(to_left[:, n, :], rl_sb[:, n, :], banks["d", n][:])

        def by_u(t):
            return t.rearrange("p (q u e) -> p u q e", u=2, e=2)

        def dz_node(a, n):
            return dz[a][:, n, :, :].rearrange("p u (q e) -> p u q e", e=2)

        def sum_a(n):
            nc.vector.tensor_tensor(
                out=dz_node(0, n), in0=by_u(to_right[:, n, :]), in1=by_u(to_left[:, n - 1, :]), op=ALU.add
            )

        def sum_c(n):
            nc.vector.tensor_tensor(
                out=dz_node(1, n), in0=by_u(to_right[:, n - 1, :]), in1=by_u(to_left[:, n, :]), op=ALU.add
            )

        end_terms = {
            (0, 0): to_right[:, 0, :],
            (1, 0): to_left[:, 0, :],
            (0, NODES - 1): to_left[:, EDGES - 1, :],
            (1, NODES - 1): to_right[:, EDGES - 1, :],
        }

        def end_node(a, n):
            nc.gpsimd.tensor_scalar(
                out=dz_node(a, n), in0=by_u(end_terms[a, n]), scalar1=1.0, scalar2=0.0, op0=ALU.mult, op1=ALU.add
            )

        f_grp = [sb.tile([P, SLOTS, 2 * P, 4], BF16, name="f_grp%d" % a, align_bytes=64) for a in range(2)]
        f_cod = [sb.tile([P, TOKENS], U32, name="f_cod%d" % a, align_bytes=64) for a in range(2)]
        f_scl = [sb.tile([P, TOKENS], U8, name="f_scl%d" % a, align_bytes=64) for a in range(2)]
        t_cod = [[sb.tile([P, F], U32, name="t_cod%d%d" % (a, x), align_bytes=64) for x in range(2)] for a in range(2)]
        t_scl = [[sb.tile([P, F], U8, name="t_scl%d%d" % (a, x), align_bytes=64) for x in range(2)] for a in range(2)]

        def filling(key):
            if key not in banks:
                banks[key] = new_bank()
            return banks[key]

        def turn_dz(a, t, n2):
            b = filling(("f", a, t))
            for u in range(2):
                c = n2 * 256 + u * P
                nc.tensor.transpose(b[:, c : c + P], dz[a][:, t + SLOTS * n2, u, :].bitcast(F32), ident[:])

        def gather_dz(a, t, engine):
            dst = merge(f_grp[a][:, t]).bitcast(F32).rearrange("q (c n u) -> q c n u", n=2, u=2)
            copy(engine, dst, banks["f", a, t][:].rearrange("q (n u c) -> q c n u", n=2, u=2))

        def quantise_features(a, t):
            c = slice(t * 2 * P, (t + 1) * 2 * P)
            quantise(f_cod[a][:, c], f_scl[a][:, c], merge(f_grp[a][:, t]), E5M2)

        t_grp = [
            [sb.tile([P, 2, F // 2, SLOTS], BF16, name="t_grp%d%d" % (a, x), align_bytes=64) for x in range(2)]
            for a in range(2)
        ]

        def turn_back(a, x, u, t):
            words = merge(f_grp[a][:, t, x * P : (x + 1) * P, :]).bitcast(F32)
            b = filling(("t", a, x, u))
            nc.tensor.transpose(b[:, t * P : (t + 1) * P], words[:, u::2], ident[:])

        def gather_tokens(a, x, u, engine):
            copy(engine, t_grp[a][x][:, u], banks["t", a, x, u][:].bitcast(BF16).rearrange("p (t n) -> p n t", t=SLOTS))

        def quantise_tokens(a, x):
            quantise(t_cod[a][x][:], t_scl[a][x][:], t_grp[a][x][:].rearrange("p u n t -> p (u n t)"), E5M2)

        h_grp = [sb.tile([P, H, SLOTS], BF16, name="h_grp%d" % x, align_bytes=64) for x in range(2)]
        h_cod = [sb.tile([P, H], U32, name="h_cod%d" % x, align_bytes=64) for x in range(2)]
        h_scl = [sb.tile([P, H], U8, name="h_scl%d" % x, align_bytes=64) for x in range(2)]

        def gather_h(x, i, engine):
            c = slice(i * P, (i + 1) * P)
            dst = h_grp[x][:, c, :].rearrange("p (c i) t -> p c t i", i=4)
            copy(engine, dst, h_sb[:, x, :, c].rearrange("p t (c i) -> p c t i", i=4))

        def quantise_h(x):
            quantise(h_cod[x][:], h_scl[x][:], merge(h_grp[x][:]), E4M3)

        out0_view = out_0.rearrange("(x c) (n t) h -> x (c n) t h", x=2, n=2)
        out1_view = out_1.rearrange("(a m p) f -> a p m f", a=2, p=P)

        def product_dx(t, x, a):
            c = slice(t * 2 * P + x * P, t * 2 * P + (x + 1) * P)
            nc.tensor.matmul_mx(
                out=filling(("dx", t, x))[:],
                lhsT=f_cod[a][:, c].bitcast(E5M2),
                lhsT_scale=f_scl[a][:, c],
                rhs=ew1_cod[a][:].bitcast(E4M3),
                rhs_scale=ew1_scl[a][:],
                start=(a == 0),
                stop=(a == 1),
            )

        def store_dx(t, x, engine):
            o = sb.tile([P, H], F32, name="dx_out", tag="dx_out", bufs=6, align_bytes=64)
            copy(engine, o[:], banks["dx", t, x][:])
            dma(out0_view[x][:, t, :], o[:])

        def product_dw(a, m, x):
            c = slice(m * P, (m + 1) * P)
            nc.tensor.matmul_mx(
                out=filling(("dw", a, m))[:],
                lhsT=h_cod[x][:, c].bitcast(E4M3),
                lhsT_scale=h_scl[x][:, c],
                rhs=t_cod[a][x][:].bitcast(E5M2),
                rhs_scale=t_scl[a][x][:],
                start=(x == 0),
                stop=(x == 1),
            )

        def store_dw(a, m, engine):
            o = sb.tile([P, F], F32, name="dw_out", tag="dw_out", bufs=6, align_bytes=64)
            dst = o[:].rearrange("p (q u e) -> p q u e", u=2, e=2)
            copy(engine, dst, banks["dw", a, m][:].rearrange("p (u q e) -> p q u e", u=2, e=2))
            dma(out1_view[a][:, m, :], o[:])

        load_ew2(0)
        load_grad(4)
        load_ew2(2)
        load_grad(2)
        load_grad(6)
        load_grad(0)
        load_lr(2)
        load_lr(4)
        turn_ew2(0)
        load_rl(3)
        load_rl(5)
        turn_grad(4)
        gather_ew2(0, SCALAR)
        load_ew1(1)
        turn_ew2(2)
        gather_grad(4, SCALAR)
        load_lr(0)
        turn_grad(2)
        gather_ew2(2, VECTOR)
        load_lr(6)
        turn_grad(6)
        load_rl(1)
        gather_grad(2, SCALAR)
        quantise_ew2()
        turn_grad(0)
        load_h(0)
        gather_grad(6, SCALAR)
        quantise_grad(2)
        quantise_grad(4)
        product_d(3)
        load_ew1(0)
        gather_grad(0, SCALAR)
        quantise_grad(6)
        load_lr(1)
        product_d(5)
        quantise_grad(0)
        mask_lr(3)
        load_rl(0)
        product_d(6)
        mask_rl(3)
        product_d(1)
        mask_lr(5)
        turn_ew1(1, 0)
        load_rl(4)
        mask_rl(5)
        load_lr(3)
        turn_ew1(1, 2)
        gather_ew1(1, 0, SCALAR)
        mask_lr(1)
        load_h(1)
        product_d(0)
        gather_ew1(1, 2, SCALAR)
        product_d(7)
        sum_c(5)
        end_node(0, 0)
        load_rl(2)
        product_d(2)
        sum_c(3)
        mask_rl(1)
        turn_dz(1, 3, 0)
        gather_h(0, 0, SCALAR)
        load_lr(5)
        product_d(4)
        sum_a(4)
        gather_h(0, 3, SCALAR)
        sum_c(1)
        turn_ew1(0, 2)
        load_rl(6)
        gather_h(0, 1, SCALAR)
        sum_a(2)
        turn_dz(0, 0, 0)
        turn_dz(0, 0, 1)
        mask_lr(7)
        gather_ew1(0, 2, SCALAR)
        mask_rl(0)
        gather_h(0, 2, SCALAR)
        turn_dz(1, 1, 0)
        end_node(1, 7)
        turn_dz(1, 1, 1)
        turn_ew1(0, 0)
        mask_rl(4)
        gather_dz(0, 0, SCALAR)
        sum_a(6)
        keep_busy_mx()
        gather_dz(1, 1, SCALAR)
        mask_lr(2)
        turn_dz(1, 3, 1)
        gather_h(1, 0, SCALAR)
        mask_lr(4)
        turn_dz(0, 2, 0)
        turn_back(0, 1, 1, 0)
        turn_back(0, 0, 0, 0)
        gather_dz(1, 3, SCALAR)
        turn_dz(0, 2, 1)
        mask_rl(2)
        turn_back(1, 1, 1, 1)
        gather_h(1, 1, SCALAR)
        turn_back(1, 1, 1, 3)
        mask_lr(6)
        turn_back(0, 0, 1, 0)
        keep_busy(4)
        gather_h(1, 2, SCALAR)
        mask_rl(6)
        sum_a(1)
        gather_ew1(0, 0, SCALAR)
        end_node(0, 7)
        sum_a(3)
        gather_dz(0, 2, SCALAR)
        end_node(1, 0)
        turn_dz(0, 1, 0)
        sum_a(5)
        gather_h(1, 3, SCALAR)
        turn_dz(0, 3, 1)
        turn_dz(0, 3, 0)
        keep_busy(1)
        sum_c(4)
        turn_back(0, 0, 1, 2)
        gather_dz(0, 3, SCALAR)
        turn_dz(0, 1, 1)
        turn_dz(1, 0, 0)
        turn_back(0, 1, 0, 0)
        sum_c(2)
        turn_back(0, 0, 0, 2)
        gather_dz(0, 1, SCALAR)
        turn_dz(1, 0, 1)
        turn_back(0, 0, 1, 3)
        turn_back(0, 0, 0, 3)
        sum_c(6)
        turn_back(1, 0, 1, 3)
        gather_dz(1, 0, SCALAR)
        turn_back(0, 0, 0, 1)
        keep_busy(2)
        quantise_ew1(0)
        gather_tokens(0, 0, 0, SCALAR)
        turn_back(0, 1, 1, 2)
        turn_dz(1, 2, 1)
        turn_dz(1, 2, 0)
        quantise_features(1, 3)
        turn_back(0, 1, 0, 3)
        turn_back(0, 1, 1, 1)
        quantise_features(0, 3)
        turn_back(0, 1, 1, 3)
        gather_dz(1, 2, SCALAR)
        turn_back(0, 0, 1, 1)
        turn_back(1, 0, 1, 0)
        quantise_features(0, 1)
        turn_back(1, 0, 0, 0)
        turn_back(1, 0, 0, 1)
        quantise_features(0, 2)
        gather_tokens(0, 0, 1, SCALAR)
        turn_back(0, 1, 0, 2)
        turn_back(0, 1, 0, 1)
        turn_back(1, 0, 0, 3)
        quantise_features(1, 1)
        turn_back(1, 0, 0, 2)
        turn_back(1, 1, 0, 3)
        quantise_ew1(1)
        turn_back(1, 1, 0, 1)
        turn_back(1, 0, 1, 2)
        gather_tokens(0, 1, 0, SCALAR)
        product_dx(3, 1, 0)
        quantise_h(0)
        product_dx(3, 0, 0)
        product_dx(3, 0, 1)
        gather_tokens(0, 1, 1, SCALAR)
        turn_back(1, 0, 1, 1)
        quantise_h(1)
        turn_back(1, 1, 0, 0)
        turn_back(1, 1, 0, 2)
        product_dx(3, 1, 1)
        quantise_features(1, 2)
        store_dx(3, 0, SCALAR)
        product_dx(1, 1, 0)
        quantise_tokens(0, 0)
        product_dx(1, 0, 0)
        store_dx(3, 1, SCALAR)
        product_dx(1, 0, 1)
        quantise_tokens(0, 1)
        product_dx(1, 1, 1)
        product_dw(0, 2, 0)
        store_dx(1, 0, SCALAR)
        gather_tokens(1, 0, 1, VECTOR)
        product_dw(0, 2, 1)
        product_dx(2, 0, 0)
        store_dx(1, 1, SCALAR)
        product_dx(2, 0, 1)
        gather_tokens(1, 1, 0, VECTOR)
        product_dw(0, 3, 0)
        store_dw(0, 2, SCALAR)
        product_dw(0, 3, 1)
        product_dw(0, 0, 0)
        store_dx(2, 0, SCALAR)
        product_dw(0, 0, 1)
        store_dw(0, 3, VECTOR)
        product_dx(2, 1, 0)
        gather_tokens(1, 0, 0, SCALAR)
        turn_back(1, 1, 1, 0)
        store_dw(0, 0, VECTOR)
        turn_back(1, 1, 1, 2)
        product_dx(2, 1, 1)
        quantise_features(1, 0)
        product_dw(0, 1, 0)
        gather_tokens(1, 1, 1, SCALAR)
        quantise_features(0, 0)
        product_dw(0, 1, 1)
        store_dx(2, 1, VECTOR)
        product_dx(0, 1, 0)
        store_dw(0, 1, SCALAR)
        product_dx(0, 0, 0)
        quantise_tokens(1, 0)
        product_dx(0, 1, 1)
        product_dx(0, 0, 1)
        quantise_tokens(1, 1)
        store_dx(0, 1, SCALAR)
        product_dw(1, 1, 0)
        product_dw(1, 2, 0)
        store_dx(0, 0, VECTOR)
        product_dw(1, 1, 1)
        product_dw(1, 0, 0)
        product_dw(1, 2, 1)
        store_dw(1, 1, VECTOR)
        product_dw(1, 0, 1)
        keep_busy_mx()
        store_dw(1, 2, VECTOR)
        product_dw(1, 3, 0)
        product_dw(1, 3, 1)
        store_dw(1, 0, VECTOR)
        store_dw(1, 3, SCALAR)
